import numpy as np
import ml_dtypes


def mxq(x, axis, fmt="e4m3"):
    dtype, down = {"e4m3": (ml_dtypes.float8_e4m3fn, 7), "e5m2": (ml_dtypes.float8_e5m2, 14)}[fmt]
    v = np.moveaxis(np.asarray(x, np.float32).astype(ml_dtypes.bfloat16).astype(np.float64), axis, -1)
    blocks = v.reshape(v.shape[:-1] + (-1, 32))
    amax = np.abs(blocks).max(-1, keepdims=True)
    byte = np.maximum(np.where(amax > 0, np.frexp(amax)[1] - 1 + 127, 0) - down, 1)
    scale = np.exp2(byte - 127.0)
    codes = (blocks / scale).astype(np.float32).astype(dtype).astype(np.float64)
    return np.moveaxis((codes * scale).reshape(v.shape), -1, axis)


WIDE = False


def mx_kscale(k):
    if not WIDE:
        return np.ones(k)
    levels = np.array([10, -10, 5, -5, 0])
    if k % 512:
        return np.exp2(np.random.permutation(np.resize(levels, k // 32))).repeat(32)
    a = np.empty((k // 512, 16))
    for p in range(k // 512):
        a[p, :8] = np.random.permutation(np.resize(levels, 8))
        for g in range(8):
            far = levels[np.abs(levels - a[p, g]) >= 10]
            a[p, g + 8] = far[np.random.randint(len(far))]
    return np.exp2(a.ravel()).repeat(32)


BF16 = ml_dtypes.bfloat16


def bf(x):
    return np.asarray(x, np.float32).astype(BF16)


def f64(x):
    return np.asarray(x).astype(np.float64)


B, T, C, H = 2, 512, 1024, 8
DH = C // H


def rope_tables():
    i = f64(np.arange(1, DH // 2 + 1))
    thetas = np.repeat(1000.0 ** (-2.0 * i / DH), 2)
    pos = f64(np.arange(1, T + 1))
    args = pos[:, None] * thetas[None, :]
    return np.sin(args), np.cos(args)


def apply_rope(u, sin, cos):
    u_odd = u[..., ::2]
    u_even = u[..., 1::2]
    u_sin = np.stack([-u_even, u_odd], axis=-1).reshape(u.shape)
    return u * cos + u_sin * sin


def setup_inputs():
    s = mx_kscale(C)
    return {"x": bf(np.random.standard_normal((B, T, C)) * s),
            "w_qk": bf(np.random.standard_normal((2 * C, C)) / np.sqrt(C) / s[None, :])}


def reference(x, w_qk):
    qk = mxq(f64(x), 2, "e4m3") @ mxq(f64(w_qk), 1, "e4m3").T
    q, k = np.split(qk, 2, axis=-1)
    q = q.reshape(B, T, H, DH).transpose(0, 2, 1, 3)
    k = k.reshape(B, T, H, DH).transpose(0, 2, 1, 3)
    sin, cos = rope_tables()
    return q, k, apply_rope(q, sin, cos), apply_rope(k, sin, cos)

@@ -1,0 +1,213 @@
+import math
+from contextlib import ExitStack
+
+import concourse.masks as masks
+import concourse.mybir as mybir
+
+F32 = mybir.dt.float32
+BF16 = mybir.dt.bfloat16
+I32 = mybir.dt.int32
+U32 = mybir.dt.uint32
+U8 = mybir.dt.uint8
+FP8X4 = mybir.dt.float8_e4m3fn_x4
+ALU = mybir.AluOpType
+ACT = mybir.ActivationFunctionType
+
+B, T, C, H, DH = 2, 512, 1024, 8, 128
+P = 128
+PACK = 4
+PASSES = C // (P * PACK)
+J = T // P
+CHUNK = 512
+CHUNKS = 2 * C // CHUNK
+ROW_TILES = CHUNK // P
+HEADS = CHUNK // DH
+PAIRS = DH // 2
+
+FLOPS = 2 * B * T * C * 2 * C
+
+RATIO = 1000.0 ** (-2.0 / DH)
+ROUND_MAGIC = 1.5 * 2.0**23
+
+
+def tile_ropeattnlayer_pa_kernel(tc, x, w_qk, out_0, out_1, out_2, out_3):
+    nc = tc.nc
+    with ExitStack() as ctx:
+        const = ctx.enter_context(tc.tile_pool(name="const", bufs=1))
+        loaded = ctx.enter_context(tc.tile_pool(name="loaded", bufs=1))
+        keep = ctx.enter_context(tc.tile_pool(name="keep", bufs=1))
+        stage = ctx.enter_context(tc.tile_pool(name="stage", bufs=4))
+        results = ctx.enter_context(tc.tile_pool(name="results", bufs=3))
+        psum_flip = ctx.enter_context(tc.psum_pool(name="psum_flip", bufs=2))
+        psum_acc = ctx.enter_context(tc.psum_pool(name="psum_acc", bufs=6))
+
+        w_tiles = w_qk.rearrange("(c t p) k -> c t p k", t=ROW_TILES, p=P)
+        x_tiles = x.rearrange("b (p j) k -> b j p k", j=J)
+        w_rows = [[None] * ROW_TILES for c in range(CHUNKS)]
+        x_rows = [[None] * J for b in range(B)]
+
+        def load_w(c):
+            for t in range(ROW_TILES):
+                w_rows[c][t] = loaded.tile([P, C], BF16, name="w_rows%d_%d" % (c, t))
+                nc.sync.dma_start(out=w_rows[c][t][:], in_=w_tiles[c, t])
+
+        def load_x(b):
+            for j in range(J):
+                x_rows[b][j] = loaded.tile([P, C], BF16, name="x_rows%d_%d" % (b, j))
+                nc.sync.dma_start(out=x_rows[b][j][:], in_=x_tiles[b, j])
+
+        load_w(0)
+        load_x(0)
+        for c in range(1, CHUNKS):
+            load_w(c)
+        load_x(1)
+
+        zero = const.tile([P, 1], F32)
+        nc.vector.memset(zero[:], 0.0)
+        warm = const.tile([P, 1], F32)
+        nc.scalar.activation(out=warm[:], in_=zero[:], func=ACT.Sin)
+
+        position_int = const.tile([P, J], I32)
+        nc.gpsimd.iota(position_int[:], pattern=[[1, J]], base=1, channel_multiplier=J)
+        ident = const.tile([P, P], F32)
+        masks.make_identity(nc, ident[:])
+        position = const.tile([P, J], F32)
+        nc.vector.tensor_copy(out=position[:], in_=position_int[:])
+        turns = const.tile([P, 2, J, PAIRS], F32)
+        nc.vector.tensor_scalar_mul(
+            out=turns[:, 1, :, 0:1], in0=position[:].unsqueeze(2), scalar1=RATIO / (2.0 * math.pi)
+        )
+        for doubling in range(6):
+            n = 2**doubling
+            nc.vector.tensor_scalar_mul(
+                out=turns[:, 1, :, n : 2 * n], in0=turns[:, 1, :, 0:n], scalar1=RATIO**n
+            )
+        nc.vector.tensor_scalar_add(out=turns[:, 0], in0=turns[:, 1], scalar1=0.25)
+        whole = const.tile([P, 2, J, PAIRS], F32)
+        nc.vector.tensor_scalar(
+            out=whole[:],
+            in0=turns[:],
+            scalar1=ROUND_MAGIC,
+            scalar2=ROUND_MAGIC,
+            op0=ALU.add,
+            op1=ALU.subtract,
+        )
+        part = const.tile([P, 2, J, PAIRS], F32)
+        nc.vector.tensor_sub(out=part[:], in0=turns[:], in1=whole[:])
+
+        table = const.tile([P, 2, J, DH], F32)
+
+        def fill_table():
+            cos_part = part[:, 0].rearrange("p j i -> p (j i)")
+            sin_part = part[:, 1].rearrange("p j i -> p (j i)")
+            cos_out = table[:, 0].rearrange("p j (i e) -> p (j i) e", e=2)
+            sin_out = table[:, 1].rearrange("p j (i e) -> p (j i) e", e=2)
+            nc.scalar.activation(
+                out=cos_out,
+                in_=cos_part.unsqueeze(2).to_broadcast([P, J * PAIRS, 2]),
+                func=ACT.Sin,
+                scale=2.0 * math.pi,
+            )
+            nc.scalar.activation(
+                out=sin_out[:, :, 0], in_=sin_part, func=ACT.Sin, scale=2.0 * math.pi
+            )
+            nc.scalar.activation(
+                out=sin_out[:, :, 1], in_=sin_part, func=ACT.Sin, scale=-2.0 * math.pi
+            )
+
+        x_codes = [
+            [keep.tile([P, PASSES, P], U32, name="x_codes%d_%d" % (b, j), align_bytes=64) for j in range(J)]
+            for b in range(B)
+        ]
+        x_scales = [
+            [keep.tile([P, PASSES, P], U8, name="x_scales%d_%d" % (b, j), align_bytes=64) for j in range(J)]
+            for b in range(B)
+        ]
+        w_codes = [
+            keep.tile([P, PASSES, CHUNK], U32, name="w_codes%d" % c, align_bytes=64) for c in range(CHUNKS)
+        ]
+        w_scales = [
+            keep.tile([P, PASSES, CHUNK], U8, name="w_scales%d" % c, align_bytes=64) for c in range(CHUNKS)
+        ]
+
+        def quantise_rows(rows, codes, scales):
+            words = rows[:].bitcast(F32)
+            flipped = psum_flip.tile([P, PASSES, 2, P], F32, tag="flipped")
+            for g in range(PASSES):
+                for u in range(2):
+                    every_second = slice(2 * P * g + u, 2 * P * (g + 1), 2)
+                    nc.tensor.transpose(flipped[:, g, u, :], words[:, every_second], ident[:])
+            grouped = stage.tile([P, PASSES * P * PACK], BF16, tag="grouped", align_bytes=64)
+            nc.scalar.copy(
+                out=grouped[:].bitcast(F32).rearrange("p (g r u) -> p g r u", g=PASSES, u=2),
+                in_=flipped[:].rearrange("p g u r -> p g r u"),
+            )
+            for g in range(PASSES):
+                nc.vector.quantize_mx(
+                    out=codes[:, g, :].bitcast(FP8X4),
+                    scales=scales[:, g, :],
+                    in_=grouped[:, g * P * PACK : (g + 1) * P * PACK],
+                )
+
+        def quantise_x(b, j):
+            quantise_rows(x_rows[b][j], x_codes[b][j][:], x_scales[b][j][:])
+
+        def quantise_w(c, t):
+            columns = slice(t * P, (t + 1) * P)
+            quantise_rows(w_rows[c][t], w_codes[c][:, :, columns], w_scales[c][:, :, columns])
+
+        def project_and_rotate(b, c, j, plain, rotated):
+            acc = psum_acc.tile([P, CHUNK], F32, tag="acc")
+            for g in range(PASSES):
+                nc.tensor.matmul_mx(
+                    out=acc[:],
+                    lhsT=x_codes[b][j][:, g, :].bitcast(FP8X4),
+                    lhsT_scale=x_scales[b][j][:, g, :],
+                    rhs=w_codes[c][:, g, :].bitcast(FP8X4),
+                    rhs_scale=w_scales[c][:, g, :],
+                    start=(g == 0),
+                    stop=(g == PASSES - 1),
+                )
+            by_head = acc[:].rearrange("p (h d) -> p h d", h=HEADS)
+            products = stage.tile([P, 2, HEADS, DH], F32, tag="products")
+            nc.vector.tensor_tensor(
+                out=products[:],
+                in0=by_head.unsqueeze(1).to_broadcast([P, 2, HEADS, DH]),
+                in1=table[:, :, j, :].unsqueeze(2).to_broadcast([P, 2, HEADS, DH]),
+                op=ALU.mult,
+            )
+            nc.scalar.copy(out=plain[:, :, j, :], in_=by_head)
+            pairs = "p h (i e) -> p h i e"
+            nc.gpsimd.tensor_tensor(
+                out=rotated[:, :, j, :].rearrange(pairs, e=2),
+                in0=products[:, 0].rearrange(pairs, e=2),
+                in1=products[:, 1].rearrange(pairs, e=2)[:, :, :, ::-1],
+                op=ALU.add,
+            )
+
+        def store(result, out, b, first_head):
+            nc.sync.dma_start(
+                out=out[b, first_head : first_head + HEADS].rearrange("h (p j) d -> p h (j d)", j=J),
+                in_=result[:].rearrange("p h j d -> p h (j d)"),
+            )
+
+        for t in range(ROW_TILES):
+            quantise_w(0, t)
+        quantise_x(0, 0)
+        fill_table()
+        for b in range(B):
+            for c in range(CHUNKS):
+                plain = results.tile([P, HEADS, J, DH], F32, tag="plain")
+                rotated = results.tile([P, HEADS, J, DH], F32, tag="rotated")
+                for j in range(J):
+                    if b == 0 and c == 0 and j + 1 < J:
+                        quantise_x(0, j + 1)
+                    if b == 0 and c + 1 < CHUNKS:
+                        quantise_w(c + 1, j)
+                    if b == 0 and c + 1 == CHUNKS:
+                        quantise_x(1, j)
+                    project_and_rotate(b, c, j, plain, rotated)
+                is_key = c // (CHUNKS // 2)
+                first_head = (c % (CHUNKS // 2)) * HEADS
+                store(plain, (out_0, out_1)[is_key], b, first_head)
+                store(rotated, (out_2, out_3)[is_key], b, first_head)

@@ -18,11 +18,9 @@ P = 128
 PACK = 4
 PASSES = C // (P * PACK)
 J = T // P
-CHUNK = 512
-CHUNKS = 2 * C // CHUNK
-ROW_TILES = CHUNK // P
-HEADS = CHUNK // DH
-PAIRS = DH // 2
+HALF = DH // 2
+BANK = J * DH
+PAIRS = 2 * H // 2
 
 FLOPS = 2 * B * T * C * 2 * C
 
@@ -36,178 +34,270 @@ def tile_ropeattnlayer_pa_kernel(tc, x, w_qk, out_0, out_1, out_2, out_3):
         const = ctx.enter_context(tc.tile_pool(name="const", bufs=1))
         loaded = ctx.enter_context(tc.tile_pool(name="loaded", bufs=1))
         keep = ctx.enter_context(tc.tile_pool(name="keep", bufs=1))
-        stage = ctx.enter_context(tc.tile_pool(name="stage", bufs=4))
-        results = ctx.enter_context(tc.tile_pool(name="results", bufs=3))
-        psum_flip = ctx.enter_context(tc.psum_pool(name="psum_flip", bufs=2))
-        psum_acc = ctx.enter_context(tc.psum_pool(name="psum_acc", bufs=6))
+        stage = ctx.enter_context(tc.tile_pool(name="stage", bufs=6))
+        results = ctx.enter_context(tc.tile_pool(name="results", bufs=5))
+        psum = ctx.enter_context(tc.psum_pool(name="psum", bufs=8))
+        ctx.enter_context(tc.manual_schedule())
 
-        w_tiles = w_qk.rearrange("(c t p) k -> c t p k", t=ROW_TILES, p=P)
-        x_tiles = x.rearrange("b (p j) k -> b j p k", j=J)
-        w_rows = [[None] * ROW_TILES for c in range(CHUNKS)]
+        w_view = w_qk.rearrange("(h p) k -> p h k", p=P)
+        x_view = x.rearrange("b (p j) k -> b p j k", j=J)
+        w_rows = [None] * (2 * H)
         x_rows = [[None] * J for b in range(B)]
 
-        def load_w(c):
-            for t in range(ROW_TILES):
-                w_rows[c][t] = loaded.tile([P, C], BF16, name="w_rows%d_%d" % (c, t))
-                nc.sync.dma_start(out=w_rows[c][t][:], in_=w_tiles[c, t])
+        def load_w(first, count):
+            tile = loaded.tile([P, count, C], BF16, name="w_rows%d" % first)
+            nc.sync.dma_start(out=tile[:], in_=w_view[:, first : first + count, :])
+            for n in range(count):
+                w_rows[first + n] = (tile, n)
 
-        def load_x(b):
-            for j in range(J):
-                x_rows[b][j] = loaded.tile([P, C], BF16, name="x_rows%d_%d" % (b, j))
-                nc.sync.dma_start(out=x_rows[b][j][:], in_=x_tiles[b, j])
+        def load_x(b, first, count):
+            tile = loaded.tile([P, count, C], BF16, name="x_rows%d_%d" % (b, first))
+            nc.sync.dma_start(out=tile[:], in_=x_view[b, :, first : first + count, :])
+            for n in range(count):
+                x_rows[b][first + n] = (tile, n)
 
-        load_w(0)
-        load_x(0)
-        for c in range(1, CHUNKS):
-            load_w(c)
-        load_x(1)
+        load_w(0, 1)
+        for j in range(J):
+            load_x(0, j, 1)
+        for h in range(1, 4):
+            load_w(h, 1)
+        for h in range(4, 2 * H, 2):
+            load_w(h, 2)
+            if h in (6, 10):
+                load_x(1, (h - 6) // 2, 2)
 
         zero = const.tile([P, 1], F32)
         nc.vector.memset(zero[:], 0.0)
         warm = const.tile([P, 1], F32)
         nc.scalar.activation(out=warm[:], in_=zero[:], func=ACT.Sin)
 
-        position_int = const.tile([P, J], I32)
-        nc.gpsimd.iota(position_int[:], pattern=[[1, J]], base=1, channel_multiplier=J)
+        position = const.tile([P, J], F32)
+        nc.gpsimd.iota(
+            position[:], pattern=[[1, J]], base=1, channel_multiplier=J, allow_small_or_imprecise_dtypes=True
+        )
         ident = const.tile([P, P], F32)
         masks.make_identity(nc, ident[:])
-        position = const.tile([P, J], F32)
-        nc.vector.tensor_copy(out=position[:], in_=position_int[:])
-        turns = const.tile([P, 2, J, PAIRS], F32)
+        turns = const.tile([P, J, HALF], F32)
         nc.vector.tensor_scalar_mul(
-            out=turns[:, 1, :, 0:1], in0=position[:].unsqueeze(2), scalar1=RATIO / (2.0 * math.pi)
+            out=turns[:, :, 0:1], in0=position[:].unsqueeze(2), scalar1=RATIO / (2.0 * math.pi)
         )
-        for doubling in range(6):
-            n = 2**doubling
-            nc.vector.tensor_scalar_mul(
-                out=turns[:, 1, :, n : 2 * n], in0=turns[:, 1, :, 0:n], scalar1=RATIO**n
-            )
-        nc.vector.tensor_scalar_add(out=turns[:, 0], in0=turns[:, 1], scalar1=0.25)
-        whole = const.tile([P, 2, J, PAIRS], F32)
+        for n in (1, 4, 16):
+            for m in range(1, 4):
+                nc.vector.tensor_scalar_mul(
+                    out=turns[:, :, m * n : (m + 1) * n], in0=turns[:, :, 0:n], scalar1=RATIO ** (m * n)
+                )
+        whole = const.tile([P, J * HALF], F32)
+        flat_turns = turns[:].rearrange("p j i -> p (j i)")
         nc.vector.tensor_scalar(
             out=whole[:],
-            in0=turns[:],
+            in0=flat_turns,
             scalar1=ROUND_MAGIC,
             scalar2=ROUND_MAGIC,
             op0=ALU.add,
             op1=ALU.subtract,
         )
-        part = const.tile([P, 2, J, PAIRS], F32)
-        nc.vector.tensor_sub(out=part[:], in0=turns[:], in1=whole[:])
+        part = const.tile([P, J * HALF], F32)
+        nc.vector.tensor_sub(out=part[:], in0=flat_turns, in1=whole[:])
+        minus_abs = const.tile([P, J * HALF], F32)
+        nc.vector.scalar_tensor_tensor(
+            out=minus_abs[:], in0=part[:], scalar=-1.0, in1=part[:], op0=ALU.mult, op1=ALU.min
+        )
+        to_quarter = const.tile([P, J * HALF], F32)
+        nc.vector.tensor_scalar_add(out=to_quarter[:], in0=minus_abs[:], scalar1=0.25)
 
-        table = const.tile([P, 2, J, DH], F32)
+        table = const.tile([P, 2, 2, J * HALF], F32)
 
         def fill_table():
-            cos_part = part[:, 0].rearrange("p j i -> p (j i)")
-            sin_part = part[:, 1].rearrange("p j i -> p (j i)")
-            cos_out = table[:, 0].rearrange("p j (i e) -> p (j i) e", e=2)
-            sin_out = table[:, 1].rearrange("p j (i e) -> p (j i) e", e=2)
-            nc.scalar.activation(
-                out=cos_out,
-                in_=cos_part.unsqueeze(2).to_broadcast([P, J * PAIRS, 2]),
-                func=ACT.Sin,
-                scale=2.0 * math.pi,
-            )
-            nc.scalar.activation(
-                out=sin_out[:, :, 0], in_=sin_part, func=ACT.Sin, scale=2.0 * math.pi
-            )
-            nc.scalar.activation(
-                out=sin_out[:, :, 1], in_=sin_part, func=ACT.Sin, scale=-2.0 * math.pi
-            )
+            for q, f, angle, sign in (
+                (0, 1, part, 1),
+                (1, 0, part, -1),
+                (0, 0, to_quarter, 1),
+                (1, 1, to_quarter, 1),
+            ):
+                nc.scalar.activation(
+                    out=table[:, q, f], in_=angle[:], func=ACT.Sin, scale=sign * 2.0 * math.pi
+                )
 
-        x_codes = [
-            [keep.tile([P, PASSES, P], U32, name="x_codes%d_%d" % (b, j), align_bytes=64) for j in range(J)]
-            for b in range(B)
-        ]
-        x_scales = [
-            [keep.tile([P, PASSES, P], U8, name="x_scales%d_%d" % (b, j), align_bytes=64) for j in range(J)]
-            for b in range(B)
-        ]
-        w_codes = [
-            keep.tile([P, PASSES, CHUNK], U32, name="w_codes%d" % c, align_bytes=64) for c in range(CHUNKS)
-        ]
-        w_scales = [
-            keep.tile([P, PASSES, CHUNK], U8, name="w_scales%d" % c, align_bytes=64) for c in range(CHUNKS)
-        ]
+        x_codes = [[None] * J for b in range(B)]
+        w_codes = [None] * (2 * H)
 
-        def quantise_rows(rows, codes, scales):
-            words = rows[:].bitcast(F32)
-            flipped = psum_flip.tile([P, PASSES, 2, P], F32, tag="flipped")
+        def flip(source, grouped, n, copy):
+            rows, m = source
+            words = rows[:, m, :].bitcast(F32)
+            flipped = psum.tile([P, PASSES, 2, P], F32, name="flipped", tag="bank")
             for g in range(PASSES):
                 for u in range(2):
                     every_second = slice(2 * P * g + u, 2 * P * (g + 1), 2)
                     nc.tensor.transpose(flipped[:, g, u, :], words[:, every_second], ident[:])
-            grouped = stage.tile([P, PASSES * P * PACK], BF16, tag="grouped", align_bytes=64)
-            nc.scalar.copy(
-                out=grouped[:].bitcast(F32).rearrange("p (g r u) -> p g r u", g=PASSES, u=2),
+            copy(
+                out=grouped[:, n, :].bitcast(F32).rearrange("p (g r u) -> p g r u", g=PASSES, u=2),
                 in_=flipped[:].rearrange("p g u r -> p g r u"),
             )
-            for g in range(PASSES):
-                nc.vector.quantize_mx(
-                    out=codes[:, g, :].bitcast(FP8X4),
-                    scales=scales[:, g, :],
-                    in_=grouped[:, g * P * PACK : (g + 1) * P * PACK],
-                )
 
-        def quantise_x(b, j):
-            quantise_rows(x_rows[b][j], x_codes[b][j][:], x_scales[b][j][:])
+        def new_grouped(tiles):
+            return stage.tile(
+                [P, tiles, PASSES * P * PACK], BF16, name="grouped", tag="grouped", align_bytes=64
+            )
 
-        def quantise_w(c, t):
-            columns = slice(t * P, (t + 1) * P)
-            quantise_rows(w_rows[c][t], w_codes[c][:, :, columns], w_scales[c][:, :, columns])
+        def quantise(grouped, tiles, name):
+            codes = keep.tile([P, tiles, PASSES, P], U32, name=name + "_codes", align_bytes=64)
+            scales = keep.tile([P, tiles, PASSES, P], U8, name=name + "_scales", align_bytes=64)
+            nc.vector.quantize_mx(
+                out=codes[:].rearrange("p n g r -> p (n g r)").bitcast(FP8X4),
+                scales=scales[:].rearrange("p n g r -> p (n g r)"),
+                in_=grouped[:].rearrange("p n c -> p (n c)"),
+            )
+            return [(codes[:, n], scales[:, n]) for n in range(tiles)]
 
-        def project_and_rotate(b, c, j, plain, rotated):
-            acc = psum_acc.tile([P, CHUNK], F32, tag="acc")
-            for g in range(PASSES):
-                nc.tensor.matmul_mx(
-                    out=acc[:],
-                    lhsT=x_codes[b][j][:, g, :].bitcast(FP8X4),
-                    lhsT_scale=x_scales[b][j][:, g, :],
-                    rhs=w_codes[c][:, g, :].bitcast(FP8X4),
-                    rhs_scale=w_scales[c][:, g, :],
-                    start=(g == 0),
-                    stop=(g == PASSES - 1),
-                )
-            by_head = acc[:].rearrange("p (h d) -> p h d", h=HEADS)
-            products = stage.tile([P, 2, HEADS, DH], F32, tag="products")
+        def project(unit):
+            b, h, j0, j1 = unit
+            acc = psum.tile([P, J, DH], F32, name="acc", tag="bank")
+            for j in range(j0, j1):
+                for g in range(PASSES):
+                    nc.tensor.matmul_mx(
+                        out=acc[:, j - j0, :],
+                        lhsT=x_codes[b][j][0][:, g, :].bitcast(FP8X4),
+                        lhsT_scale=x_codes[b][j][1][:, g, :],
+                        rhs=w_codes[h][0][:, g, :].bitcast(FP8X4),
+                        rhs_scale=w_codes[h][1][:, g, :],
+                        start=(g == 0),
+                        stop=(g == PASSES - 1),
+                    )
+            return acc
+
+        def multiply(unit, acc):
+            b, h, j0, j1 = unit
+            n = (j1 - j0) * HALF
+            products = stage.tile([P, 2, n, 2], F32, name="products", tag="products")
+            by_parity = acc[:, 0 : j1 - j0, :].rearrange("p j (i q) -> p q (j i)", q=2)
             nc.vector.tensor_tensor(
                 out=products[:],
-                in0=by_head.unsqueeze(1).to_broadcast([P, 2, HEADS, DH]),
-                in1=table[:, :, j, :].unsqueeze(2).to_broadcast([P, 2, HEADS, DH]),
+                in0=by_parity.unsqueeze(3).to_broadcast([P, 2, n, 2]),
+                in1=table[:, :, :, j0 * HALF : j1 * HALF].rearrange("p q f n -> p q n f"),
                 op=ALU.mult,
             )
-            nc.scalar.copy(out=plain[:, :, j, :], in_=by_head)
-            pairs = "p h (i e) -> p h i e"
-            nc.gpsimd.tensor_tensor(
-                out=rotated[:, :, j, :].rearrange(pairs, e=2),
-                in0=products[:, 0].rearrange(pairs, e=2),
-                in1=products[:, 1].rearrange(pairs, e=2)[:, :, :, ::-1],
+            return products
+
+        def add(engine, products, rotated):
+            engine.tensor_tensor(
+                out=rotated,
+                in0=products[:, 0].rearrange("p n f -> p (n f)"),
+                in1=products[:, 1].rearrange("p n f -> p (n f)"),
                 op=ALU.add,
             )
 
         def store(result, out, b, first_head):
             nc.sync.dma_start(
-                out=out[b, first_head : first_head + HEADS].rearrange("h (p j) d -> p h (j d)", j=J),
-                in_=result[:].rearrange("p h j d -> p h (j d)"),
+                out=out[b, first_head : first_head + 2].rearrange("h (p j) d -> p h (j d)", j=J),
+                in_=result[:],
             )
 
-        for t in range(ROW_TILES):
-            quantise_w(0, t)
-        quantise_x(0, 0)
+        banks = [(b, h) for b in range(B) for h in range(2 * H)]
+        units = []
+        for b, h in banks:
+            if (b, h) in (banks[0], banks[-1]):
+                units += [(b, h, 0, J // 2), (b, h, J // 2, J)]
+            else:
+                units.append((b, h, 0, J))
+
+        scalar_copy = nc.scalar.copy
+        vector_copy = nc.vector.tensor_copy
+        accs = []
+        grouped_of = {}
+
+        def rows_of(tile):
+            return w_rows[tile[1]] if tile[0] == "w" else x_rows[tile[1]][tile[2]]
+
+        def do_flip(group, n, copy):
+            if n == 0:
+                grouped_of[group] = new_grouped(len(group))
+            flip(rows_of(group[n]), grouped_of[group], n, copy)
+
+        def do_quantise(group):
+            name = "_".join(str(part) for tile in group for part in tile)
+            made = quantise(grouped_of[group], len(group), name)
+            for n in range(len(group)):
+                tile = group[n]
+                if tile[0] == "w":
+                    w_codes[tile[1]] = made[n]
+                else:
+                    x_codes[tile[1]][tile[2]] = made[n]
+
+        def w_group(first, count):
+            return tuple(("w", first + n) for n in range(count))
+
+        def x_group(b, first, count):
+            return tuple(("x", b, first + n) for n in range(count))
+
+        do_flip(w_group(0, 1), 0, scalar_copy)
         fill_table()
-        for b in range(B):
-            for c in range(CHUNKS):
-                plain = results.tile([P, HEADS, J, DH], F32, tag="plain")
-                rotated = results.tile([P, HEADS, J, DH], F32, tag="rotated")
-                for j in range(J):
-                    if b == 0 and c == 0 and j + 1 < J:
-                        quantise_x(0, j + 1)
-                    if b == 0 and c + 1 < CHUNKS:
-                        quantise_w(c + 1, j)
-                    if b == 0 and c + 1 == CHUNKS:
-                        quantise_x(1, j)
-                    project_and_rotate(b, c, j, plain, rotated)
-                is_key = c // (CHUNKS // 2)
-                first_head = (c % (CHUNKS // 2)) * HEADS
+        do_flip(x_group(0, 0, 1), 0, vector_copy)
+        do_flip(x_group(0, 1, 1), 0, scalar_copy)
+        do_quantise(w_group(0, 1))
+        do_quantise(x_group(0, 0, 1))
+        do_flip(x_group(0, 2, 1), 0, vector_copy)
+        do_quantise(x_group(0, 1, 1))
+        do_flip(x_group(0, 3, 1), 0, scalar_copy)
+        accs.append(project(units[0]))
+        do_flip(w_group(1, 1), 0, scalar_copy)
+        do_flip(w_group(2, 1), 0, scalar_copy)
+
+        flips = {}
+        quants = {0: [x_group(0, 2, 1), x_group(0, 3, 1), w_group(1, 1)], 1: [w_group(2, 1)]}
+
+        def plan(group, flip_slot, quantise_slot):
+            flips.setdefault(flip_slot, []).append((group, 0))
+            quants.setdefault(quantise_slot, []).append(group)
+
+        for h in range(3, 2 * H):
+            plan(w_group(h, 1), h - 3, h - 1)
+        for j in range(J):
+            plan(x_group(1, j, 1), 3 * j + 3, 3 * j + 5)
+
+        def ready(unit):
+            b, h, j0, j1 = unit
+            return w_codes[h] is not None and all(x_codes[b][j] is not None for j in range(j0, j1))
+
+        results_of = {}
+
+        def result_tiles(unit):
+            b, h = unit[0], unit[1]
+            key = (b, h // 2)
+            if key not in results_of:
+                plain = results.tile([P, 2, BANK], F32, name="plain", tag="plain")
+                rotated = results.tile([P, 2, BANK], F32, name="rotated", tag="rotated")
+                results_of[key] = (plain, rotated)
+            return results_of[key]
+
+        def columns(unit):
+            return slice(unit[2] * DH, unit[3] * DH)
+
+        def finish_plain(k):
+            unit = units[k]
+            plain, rotated = result_tiles(unit)
+            b, h, j0, j1 = unit
+            nc.scalar.copy(
+                out=plain[:, h % 2, columns(unit)],
+                in_=accs[k][:, 0 : j1 - j0, :].rearrange("p j d -> p (j d)"),
+            )
+            if h % 2 == 1 and j1 == J:
+                is_key = h // H
+                first_head = (h - 1) % H
                 store(plain, (out_0, out_1)[is_key], b, first_head)
                 store(rotated, (out_2, out_3)[is_key], b, first_head)
+
+        for k in range(len(units)):
+            unit = units[k]
+            plain, rotated = result_tiles(unit)
+            for group, n in flips.get(k, []):
+                do_flip(group, n, scalar_copy)
+            products = multiply(unit, accs[k])
+            last = k == len(units) - 1
+            add(nc.vector if last else nc.gpsimd, products, rotated[:, unit[1] % 2, columns(unit)])
+            for group in quants.get(k, []):
+                do_quantise(group)
+            while len(accs) < len(units) and len(accs) <= k + 2 and ready(units[len(accs)]):
+                accs.append(project(units[len(accs)]))
+            if k > 0:
+                finish_plain(k - 1)
+        finish_plain(len(units) - 1)

@@ -34,7 +34,7 @@ def tile_ropeattnlayer_pa_kernel(tc, x, w_qk, out_0, out_1, out_2, out_3):
         const = ctx.enter_context(tc.tile_pool(name="const", bufs=1))
         loaded = ctx.enter_context(tc.tile_pool(name="loaded", bufs=1))
         keep = ctx.enter_context(tc.tile_pool(name="keep", bufs=1))
-        stage = ctx.enter_context(tc.tile_pool(name="stage", bufs=6))
+        stage = ctx.enter_context(tc.tile_pool(name="stage", bufs=5))
         results = ctx.enter_context(tc.tile_pool(name="results", bufs=5))
         psum = ctx.enter_context(tc.psum_pool(name="psum", bufs=8))
         ctx.enter_context(tc.manual_schedule())
@@ -149,13 +149,12 @@ def tile_ropeattnlayer_pa_kernel(tc, x, w_qk, out_0, out_1, out_2, out_3):
             )
             return [(codes[:, n], scales[:, n]) for n in range(tiles)]
 
-        def project(unit):
-            b, h, j0, j1 = unit
+        def project(b, h, tiles):
             acc = psum.tile([P, J, DH], F32, name="acc", tag="bank")
-            for j in range(j0, j1):
+            for j in tiles:
                 for g in range(PASSES):
                     nc.tensor.matmul_mx(
-                        out=acc[:, j - j0, :],
+                        out=acc[:, j, :],
                         lhsT=x_codes[b][j][0][:, g, :].bitcast(FP8X4),
                         lhsT_scale=x_codes[b][j][1][:, g, :],
                         rhs=w_codes[h][0][:, g, :].bitcast(FP8X4),
@@ -165,55 +164,74 @@ def tile_ropeattnlayer_pa_kernel(tc, x, w_qk, out_0, out_1, out_2, out_3):
                     )
             return acc
 
-        def multiply(unit, acc):
-            b, h, j0, j1 = unit
+        results_of = {}
+
+        def tiles_of(b, h):
+            key = (b, h // 2)
+            if key not in results_of:
+                plain = results.tile([P, 2, BANK], F32, name="plain", tag="plain")
+                rotated = results.tile([P, 2, BANK], F32, name="rotated", tag="rotated")
+                products = results.tile([P, 2, 2, BANK], F32, name="products", tag="products")
+                results_of[key] = (plain, rotated, products)
+            return results_of[key]
+
+        def multiply(b, h, acc, j0, j1):
+            products = tiles_of(b, h)[2]
             n = (j1 - j0) * HALF
-            products = stage.tile([P, 2, n, 2], F32, name="products", tag="products")
-            by_parity = acc[:, 0 : j1 - j0, :].rearrange("p j (i q) -> p q (j i)", q=2)
+            by_parity = acc[:, j0:j1, :].rearrange("p j (i q) -> p q (j i)", q=2)
             nc.vector.tensor_tensor(
-                out=products[:],
+                out=products[:, h % 2, :, j0 * DH : j1 * DH].rearrange("p q (n f) -> p q n f", f=2),
                 in0=by_parity.unsqueeze(3).to_broadcast([P, 2, n, 2]),
                 in1=table[:, :, :, j0 * HALF : j1 * HALF].rearrange("p q f n -> p q n f"),
                 op=ALU.mult,
             )
-            return products
 
-        def add(engine, products, rotated):
+        def add(engine, b, h, j0, j1):
+            plain, rotated, products = tiles_of(b, h)
+            span = slice(j0 * DH, j1 * DH)
             engine.tensor_tensor(
-                out=rotated,
-                in0=products[:, 0].rearrange("p n f -> p (n f)"),
-                in1=products[:, 1].rearrange("p n f -> p (n f)"),
+                out=rotated[:, h % 2, span],
+                in0=products[:, h % 2, 0, span],
+                in1=products[:, h % 2, 1, span],
                 op=ALU.add,
             )
 
-        def store(result, out, b, first_head):
-            nc.sync.dma_start(
-                out=out[b, first_head : first_head + 2].rearrange("h (p j) d -> p h (j d)", j=J),
-                in_=result[:],
+        def add_on_tensor(b, h):
+            products = tiles_of(b, h)[2]
+            total = psum.tile([P, BANK], F32, name="total", tag="bank")
+            for q in range(2):
+                nc.tensor.matmul(
+                    total[:], lhsT=ident[:], rhs=products[:, h % 2, q, :], start=(q == 0), stop=(q == 1)
+                )
+            return total
+
+        def copy_plain(b, h, acc, j0, j1):
+            plain = tiles_of(b, h)[0]
+            nc.scalar.copy(
+                out=plain[:, h % 2, j0 * DH : j1 * DH], in_=acc[:, j0:j1, :].rearrange("p j d -> p (j d)")
             )
 
-        banks = [(b, h) for b in range(B) for h in range(2 * H)]
-        units = []
-        for b, h in banks:
-            if (b, h) in (banks[0], banks[-1]):
-                units += [(b, h, 0, J // 2), (b, h, J // 2, J)]
-            else:
-                units.append((b, h, 0, J))
+        def store(kind, b, first, count):
+            result = tiles_of(b, first)[kind]
+            out = ((out_0, out_1), (out_2, out_3))[kind][first // H]
+            to = first % H
+            nc.sync.dma_start(
+                out=out[b, to : to + count].rearrange("h (p j) d -> p h (j d)", j=J),
+                in_=result[:, first % 2 : first % 2 + count, :],
+            )
 
         scalar_copy = nc.scalar.copy
         vector_copy = nc.vector.tensor_copy
-        accs = []
         grouped_of = {}
 
-        def rows_of(tile):
-            return w_rows[tile[1]] if tile[0] == "w" else x_rows[tile[1]][tile[2]]
-
-        def do_flip(group, n, copy):
+        def flip_tile(tile, group, copy):
+            n = group.index(tile)
             if n == 0:
                 grouped_of[group] = new_grouped(len(group))
-            flip(rows_of(group[n]), grouped_of[group], n, copy)
+            rows = w_rows[tile[1]] if tile[0] == "w" else x_rows[tile[1]][tile[2]]
+            flip(rows, grouped_of[group], n, copy)
 
-        def do_quantise(group):
+        def quantise_group(group):
             name = "_".join(str(part) for tile in group for part in tile)
             made = quantise(grouped_of[group], len(group), name)
             for n in range(len(group)):
@@ -229,75 +247,136 @@ def tile_ropeattnlayer_pa_kernel(tc, x, w_qk, out_0, out_1, out_2, out_3):
         def x_group(b, first, count):
             return tuple(("x", b, first + n) for n in range(count))
 
-        do_flip(w_group(0, 1), 0, scalar_copy)
+        x0 = [x_group(0, j, 1) for j in range(J)]
+        x1 = x_group(1, 0, J)
+        w_groups = [w_group(h, 1) for h in range(4)] + [w_group(4, 2), w_group(6, 2), w_group(8, 4), w_group(12, 4)]
+
+        def flip_w(h, copy):
+            group = [group for group in w_groups if ("w", h) in group][0]
+            flip_tile(("w", h), group, copy)
+
+        flip_w(0, scalar_copy)
         fill_table()
-        do_flip(x_group(0, 0, 1), 0, vector_copy)
-        do_flip(x_group(0, 1, 1), 0, scalar_copy)
-        do_quantise(w_group(0, 1))
-        do_quantise(x_group(0, 0, 1))
-        do_flip(x_group(0, 2, 1), 0, vector_copy)
-        do_quantise(x_group(0, 1, 1))
-        do_flip(x_group(0, 3, 1), 0, scalar_copy)
-        accs.append(project(units[0]))
-        do_flip(w_group(1, 1), 0, scalar_copy)
-        do_flip(w_group(2, 1), 0, scalar_copy)
+        flip_tile(x0[0][0], x0[0], vector_copy)
+        flip_tile(x0[1][0], x0[1], scalar_copy)
+        quantise_group(w_groups[0])
+        quantise_group(x0[0])
+        flip_tile(x0[2][0], x0[2], vector_copy)
+        quantise_group(x0[1])
+        flip_tile(x0[3][0], x0[3], scalar_copy)
+        first_acc = project(0, 0, (0, 1))
+        flip_w(1, scalar_copy)
+        flip_w(2, scalar_copy)
+        multiply(0, 0, first_acc, 0, 2)
+        flip_w(3, scalar_copy)
+        quantise_group(x0[2])
+        quantise_group(x0[3])
+        second_acc = project(0, 0, (2, 3))
+        quantise_group(w_groups[1])
+        add(nc.vector, 0, 0, 0, 2)
+        flip_w(4, scalar_copy)
+        multiply(0, 0, second_acc, 2, 4)
+        quantise_group(w_groups[2])
+        add(nc.vector, 0, 0, 2, 4)
+        copy_plain(0, 0, first_acc, 0, 2)
+        copy_plain(0, 0, second_acc, 2, 4)
 
-        flips = {}
-        quants = {0: [x_group(0, 2, 1), x_group(0, 3, 1), w_group(1, 1)], 1: [w_group(2, 1)]}
+        banks = [(b, h) for b in range(B) for h in range(2 * H)][1:]
+        accs = {}
 
-        def plan(group, flip_slot, quantise_slot):
-            flips.setdefault(flip_slot, []).append((group, 0))
-            quants.setdefault(quantise_slot, []).append(group)
+        windows = {
+            1: (w_groups[3], 1),
+            2: (w_groups[4], None),
+            4: (w_groups[5], 3),
+            6: (w_groups[6], 5),
+            10: (w_groups[7], 9),
+            14: (x1, 13),
+        }
+        vector_sums = [(0, 1), (0, 3), (0, 5), (0, 9), (0, 13), (1, 15)]
+        tensor_sums = [(1, 2), (1, 7)]
+        flips = {
+            1: [5],
+            2: [6, 7],
+            3: [8],
+            4: [9, 10],
+            5: [11],
+            6: [12],
+            7: [13],
+            8: [14],
+            9: [15],
+        }
+        x1_flips = {10: 0, 11: 1, 12: 2, 13: 3}
+        added = set()
+        added.add((0, 0))
+        last_pair = [(B - 1, 2 * H - 2), (B - 1, 2 * H - 1)]
+        totals = {}
+        later = {}
 
-        for h in range(3, 2 * H):
-            plan(w_group(h, 1), h - 3, h - 1)
-        for j in range(J):
-            plan(x_group(1, j, 1), 3 * j + 3, 3 * j + 5)
+        def rotated_done(b, h):
+            added.add((b, h))
+            if (b, h) in last_pair:
+                store(1, b, h, 1)
+            elif (b, h - h % 2) in added and (b, h - h % 2 + 1) in added:
+                store(1, b, h - h % 2, 2)
 
-        def ready(unit):
-            b, h, j0, j1 = unit
-            return w_codes[h] is not None and all(x_codes[b][j] is not None for j in range(j0, j1))
+        def ready(b, h):
+            return w_codes[h] is not None and x_codes[b][J - 1] is not None
 
-        results_of = {}
+        def project_ahead(k):
+            ahead = 2 if banks[k][0] == 0 else 4
+            while len(accs) < len(banks) and len(accs) <= k + ahead and ready(*banks[len(accs)]):
+                b, h = banks[len(accs)]
+                accs[(b, h)] = project(b, h, range(J))
 
-        def result_tiles(unit):
-            b, h = unit[0], unit[1]
-            key = (b, h // 2)
-            if key not in results_of:
-                plain = results.tile([P, 2, BANK], F32, name="plain", tag="plain")
-                rotated = results.tile([P, 2, BANK], F32, name="rotated", tag="rotated")
-                results_of[key] = (plain, rotated)
-            return results_of[key]
-
-        def columns(unit):
-            return slice(unit[2] * DH, unit[3] * DH)
-
-        def finish_plain(k):
-            unit = units[k]
-            plain, rotated = result_tiles(unit)
-            b, h, j0, j1 = unit
-            nc.scalar.copy(
-                out=plain[:, h % 2, columns(unit)],
-                in_=accs[k][:, 0 : j1 - j0, :].rearrange("p j d -> p (j d)"),
-            )
-            if h % 2 == 1 and j1 == J:
-                is_key = h // H
-                first_head = (h - 1) % H
-                store(plain, (out_0, out_1)[is_key], b, first_head)
-                store(rotated, (out_2, out_3)[is_key], b, first_head)
-
-        for k in range(len(units)):
-            unit = units[k]
-            plain, rotated = result_tiles(unit)
-            for group, n in flips.get(k, []):
-                do_flip(group, n, scalar_copy)
-            products = multiply(unit, accs[k])
-            last = k == len(units) - 1
-            add(nc.vector if last else nc.gpsimd, products, rotated[:, unit[1] % 2, columns(unit)])
-            for group in quants.get(k, []):
-                do_quantise(group)
-            while len(accs) < len(units) and len(accs) <= k + 2 and ready(units[len(accs)]):
-                accs.append(project(units[len(accs)]))
+        project_ahead(-1)
+        for k in range(len(banks)):
+            b, h = banks[k]
+            if b == 0:
+                for n in flips.get(h, []):
+                    flip_w(n, scalar_copy)
+                if h in x1_flips:
+                    flip_tile(x1[x1_flips[h]], x1, scalar_copy)
+            acc = accs[(b, h)]
+            window = windows.get(h) if b == 0 else None
+            last = k == len(banks) - 1
+            if last:
+                multiply(b, h, acc, 0, 2)
+                multiply(b, h, acc, 2, 4)
+                add(nc.vector, b, h, 0, 2)
+                add(nc.vector, b, h, 2, 4)
+                rotated_done(b, h)
+            elif window is None:
+                multiply(b, h, acc, 0, J)
+            else:
+                multiply(b, h, acc, 0, J - 1)
+                quantise_group(window[0])
+                if window[1] is not None and window[1] != h:
+                    add(nc.vector, b, window[1], 0, J)
+                    rotated_done(b, window[1])
+                multiply(b, h, acc, J - 1, J)
+                if window[1] == h:
+                    add(nc.vector, b, h, 0, J)
+                    rotated_done(b, h)
+            if (b, h) in tensor_sums:
+                later.setdefault(k + 2, []).append((0, b, h))
+                later.setdefault(k + 4, []).append((1, b, h))
+            elif (b, h) not in vector_sums:
+                add(nc.gpsimd, b, h, 0, J)
+                rotated_done(b, h)
+            project_ahead(k)
+            for step, bb, hh in later.get(k, []):
+                if step == 0:
+                    totals[(bb, hh)] = add_on_tensor(bb, hh)
+                else:
+                    rotated = tiles_of(bb, hh)[1]
+                    nc.scalar.copy(out=rotated[:, hh % 2, :], in_=totals[(bb, hh)][:])
+                    rotated_done(bb, hh)
             if k > 0:
-                finish_plain(k - 1)
-        finish_plain(len(units) - 1)
+                bb, hh = banks[k - 1]
+                copy_plain(bb, hh, accs[(bb, hh)], 0, J)
+                if (bb, hh) in last_pair:
+                    store(0, bb, hh, 1)
+                elif hh % 2 == 1:
+                    store(0, bb, hh - 1, 2)
+        copy_plain(b, h, acc, 0, J)
+        store(0, b, h, 1)

@@ -17,10 +17,12 @@ B, T, C, H, DH = 2, 512, 1024, 8, 128
 P = 128
 PACK = 4
 PASSES = C // (P * PACK)
-J = T // P
+ROWS = P // B
+J = T // ROWS
+GROUP = J // 2
 HALF = DH // 2
-BANK = J * DH
-PAIRS = 2 * H // 2
+BANK = GROUP * DH
+HEADS = 2 * H
 
 FLOPS = 2 * B * T * C * 2 * C
 
@@ -35,14 +37,13 @@ def tile_ropeattnlayer_pa_kernel(tc, x, w_qk, out_0, out_1, out_2, out_3):
         loaded = ctx.enter_context(tc.tile_pool(name="loaded", bufs=1))
         keep = ctx.enter_context(tc.tile_pool(name="keep", bufs=1))
         stage = ctx.enter_context(tc.tile_pool(name="stage", bufs=5))
-        results = ctx.enter_context(tc.tile_pool(name="results", bufs=5))
+        results = ctx.enter_context(tc.tile_pool(name="results", bufs=6))
         psum = ctx.enter_context(tc.psum_pool(name="psum", bufs=8))
         ctx.enter_context(tc.manual_schedule())
 
         w_view = w_qk.rearrange("(h p) k -> p h k", p=P)
-        x_view = x.rearrange("b (p j) k -> b p j k", j=J)
-        w_rows = [None] * (2 * H)
-        x_rows = [[None] * J for b in range(B)]
+        w_rows = [None] * HEADS
+        x_rows = [None] * J
 
         def load_w(first, count):
             tile = loaded.tile([P, count, C], BF16, name="w_rows%d" % first)
@@ -50,36 +51,48 @@ def tile_ropeattnlayer_pa_kernel(tc, x, w_qk, out_0, out_1, out_2, out_3):
             for n in range(count):
                 w_rows[first + n] = (tile, n)
 
-        def load_x(b, first, count):
-            tile = loaded.tile([P, count, C], BF16, name="x_rows%d_%d" % (b, first))
-            nc.sync.dma_start(out=tile[:], in_=x_view[b, :, first : first + count, :])
+        def load_x(first, count):
+            tile = loaded.tile([P, count, C], BF16, name="x_rows%d" % first)
+            for b in range(B):
+                positions = x[b].rearrange("(p j) k -> p j k", j=J)
+                nc.sync.dma_start(out=tile[b:P:B], in_=positions[:, first : first + count, :])
             for n in range(count):
-                x_rows[b][first + n] = (tile, n)
+                x_rows[first + n] = (tile, n)
 
         load_w(0, 1)
-        for j in range(J):
-            load_x(0, j, 1)
-        for h in range(1, 4):
-            load_w(h, 1)
-        for h in range(4, 2 * H, 2):
+        load_x(0, 2)
+        load_x(2, 2)
+        load_w(1, 1)
+        load_x(4, 2)
+        load_x(6, 2)
+        for h in range(2, HEADS, 2):
             load_w(h, 2)
-            if h in (6, 10):
-                load_x(1, (h - 6) // 2, 2)
 
         zero = const.tile([P, 1], F32)
         nc.vector.memset(zero[:], 0.0)
         warm = const.tile([P, 1], F32)
         nc.scalar.activation(out=warm[:], in_=zero[:], func=ACT.Sin)
 
-        position = const.tile([P, J], F32)
+        four_p = const.tile([P, 1], I32)
+        nc.gpsimd.iota(four_p[:], pattern=[[0, 1]], base=0, channel_multiplier=4)
+        tile_number = const.tile([P, J], F32)
         nc.gpsimd.iota(
-            position[:], pattern=[[1, J]], base=1, channel_multiplier=J, allow_small_or_imprecise_dtypes=True
+            tile_number[:], pattern=[[1, J]], base=1, channel_multiplier=0, allow_small_or_imprecise_dtypes=True
         )
         ident = const.tile([P, P], F32)
         masks.make_identity(nc, ident[:])
+        first_int = const.tile([P, 1], I32)
+        nc.vector.tensor_single_scalar(out=first_int[:], in_=four_p[:], scalar=T - J, op=ALU.bitwise_and)
+        first_position = const.tile([P, 1], F32)
+        nc.vector.tensor_copy(out=first_position[:], in_=first_int[:])
         turns = const.tile([P, J, HALF], F32)
-        nc.vector.tensor_scalar_mul(
-            out=turns[:, :, 0:1], in0=position[:].unsqueeze(2), scalar1=RATIO / (2.0 * math.pi)
+        nc.vector.tensor_scalar(
+            out=turns[:, :, 0:1],
+            in0=tile_number[:].unsqueeze(2),
+            scalar1=first_position[:],
+            scalar2=RATIO / (2.0 * math.pi),
+            op0=ALU.add,
+            op1=ALU.mult,
         )
         for n in (1, 4, 16):
             for m in range(1, 4):
@@ -96,30 +109,29 @@ def tile_ropeattnlayer_pa_kernel(tc, x, w_qk, out_0, out_1, out_2, out_3):
             op0=ALU.add,
             op1=ALU.subtract,
         )
-        part = const.tile([P, J * HALF], F32)
-        nc.vector.tensor_sub(out=part[:], in0=flat_turns, in1=whole[:])
+        angles = const.tile([P, 4, J * HALF], F32)
+        nc.vector.tensor_sub(out=angles[:, 1], in0=flat_turns, in1=whole[:])
+        nc.vector.tensor_scalar_mul(out=angles[:, 2], in0=angles[:, 1], scalar1=-1.0)
         minus_abs = const.tile([P, J * HALF], F32)
         nc.vector.scalar_tensor_tensor(
-            out=minus_abs[:], in0=part[:], scalar=-1.0, in1=part[:], op0=ALU.mult, op1=ALU.min
+            out=minus_abs[:], in0=angles[:, 1], scalar=-1.0, in1=angles[:, 1], op0=ALU.mult, op1=ALU.min
         )
-        to_quarter = const.tile([P, J * HALF], F32)
-        nc.vector.tensor_scalar_add(out=to_quarter[:], in0=minus_abs[:], scalar1=0.25)
+        nc.vector.tensor_scalar_add(out=angles[:, 0], in0=minus_abs[:], scalar1=0.25)
+        nc.vector.tensor_scalar_add(out=angles[:, 3], in0=minus_abs[:], scalar1=0.25)
 
-        table = const.tile([P, 2, 2, J * HALF], F32)
+        table = const.tile([P, 2, J * HALF, 2], F32)
 
-        def fill_table():
-            for q, f, angle, sign in (
-                (0, 1, part, 1),
-                (1, 0, part, -1),
-                (0, 0, to_quarter, 1),
-                (1, 1, to_quarter, 1),
-            ):
-                nc.scalar.activation(
-                    out=table[:, q, f], in_=angle[:], func=ACT.Sin, scale=sign * 2.0 * math.pi
-                )
+        def fill_table(group):
+            span = slice(group * GROUP * HALF, (group + 1) * GROUP * HALF)
+            nc.scalar.activation(
+                out=table[:, :, span, :],
+                in_=angles[:, :, span].rearrange("p (q f) n -> p q n f", q=2),
+                func=ACT.Sin,
+                scale=2.0 * math.pi,
+            )
 
-        x_codes = [[None] * J for b in range(B)]
-        w_codes = [None] * (2 * H)
+        x_codes = [None] * J
+        w_codes = [None] * HEADS
 
         def flip(source, grouped, n, copy):
             rows, m = source
@@ -149,14 +161,14 @@ def tile_ropeattnlayer_pa_kernel(tc, x, w_qk, out_0, out_1, out_2, out_3):
             )
             return [(codes[:, n], scales[:, n]) for n in range(tiles)]
 
-        def project(b, h, tiles):
-            acc = psum.tile([P, J, DH], F32, name="acc", tag="bank")
-            for j in tiles:
+        def project(h, j0, j1):
+            acc = psum.tile([P, GROUP, DH], F32, name="acc", tag="bank")
+            for j in range(j0, j1):
                 for g in range(PASSES):
                     nc.tensor.matmul_mx(
-                        out=acc[:, j, :],
-                        lhsT=x_codes[b][j][0][:, g, :].bitcast(FP8X4),
-                        lhsT_scale=x_codes[b][j][1][:, g, :],
+                        out=acc[:, j % GROUP, :],
+                        lhsT=x_codes[j][0][:, g, :].bitcast(FP8X4),
+                        lhsT_scale=x_codes[j][1][:, g, :],
                         rhs=w_codes[h][0][:, g, :].bitcast(FP8X4),
                         rhs_scale=w_codes[h][1][:, g, :],
                         start=(g == 0),
@@ -166,217 +178,169 @@ def tile_ropeattnlayer_pa_kernel(tc, x, w_qk, out_0, out_1, out_2, out_3):
 
         results_of = {}
 
-        def tiles_of(b, h):
-            key = (b, h // 2)
-            if key not in results_of:
-                plain = results.tile([P, 2, BANK], F32, name="plain", tag="plain")
-                rotated = results.tile([P, 2, BANK], F32, name="rotated", tag="rotated")
+        def tiles_of(h):
+            if h not in results_of:
+                plain = results.tile([P, J * DH], F32, name="plain", tag="plain")
+                rotated = results.tile([P, J * DH], F32, name="rotated", tag="rotated")
                 products = results.tile([P, 2, 2, BANK], F32, name="products", tag="products")
-                results_of[key] = (plain, rotated, products)
-            return results_of[key]
+                results_of[h] = (plain, rotated, products)
+            return results_of[h]
 
-        def multiply(b, h, acc, j0, j1):
-            products = tiles_of(b, h)[2]
+        def multiply(h, acc, j0, j1):
+            products = tiles_of(h)[2][:, j0 // GROUP]
             n = (j1 - j0) * HALF
-            by_parity = acc[:, j0:j1, :].rearrange("p j (i q) -> p q (j i)", q=2)
+            first = j0 % GROUP
+            span = slice(first * DH, (first + j1 - j0) * DH)
+            by_parity = acc[:, first : first + j1 - j0, :].rearrange("p j (i q) -> p q (j i)", q=2)
             nc.vector.tensor_tensor(
-                out=products[:, h % 2, :, j0 * DH : j1 * DH].rearrange("p q (n f) -> p q n f", f=2),
+                out=products[:, :, span].rearrange("p q (n f) -> p q n f", f=2),
                 in0=by_parity.unsqueeze(3).to_broadcast([P, 2, n, 2]),
-                in1=table[:, :, :, j0 * HALF : j1 * HALF].rearrange("p q f n -> p q n f"),
+                in1=table[:, :, j0 * HALF : j1 * HALF, :],
                 op=ALU.mult,
             )
 
-        def add(engine, b, h, j0, j1):
-            plain, rotated, products = tiles_of(b, h)
-            span = slice(j0 * DH, j1 * DH)
+        def add(engine, h, j0, j1):
+            plain, rotated, products = tiles_of(h)
+            half = j0 // GROUP
+            span = slice((j0 - half * GROUP) * DH, (j1 - half * GROUP) * DH)
             engine.tensor_tensor(
-                out=rotated[:, h % 2, span],
-                in0=products[:, h % 2, 0, span],
-                in1=products[:, h % 2, 1, span],
+                out=rotated[:, j0 * DH : j1 * DH],
+                in0=products[:, half, 0, span],
+                in1=products[:, half, 1, span],
                 op=ALU.add,
             )
 
-        def add_on_tensor(b, h):
-            products = tiles_of(b, h)[2]
-            total = psum.tile([P, BANK], F32, name="total", tag="bank")
-            for q in range(2):
-                nc.tensor.matmul(
-                    total[:], lhsT=ident[:], rhs=products[:, h % 2, q, :], start=(q == 0), stop=(q == 1)
-                )
-            return total
-
-        def copy_plain(b, h, acc, j0, j1):
-            plain = tiles_of(b, h)[0]
+        def copy_plain(h, acc, j0, j1):
+            plain = tiles_of(h)[0]
+            first = j0 % GROUP
             nc.scalar.copy(
-                out=plain[:, h % 2, j0 * DH : j1 * DH], in_=acc[:, j0:j1, :].rearrange("p j d -> p (j d)")
+                out=plain[:, j0 * DH : j1 * DH],
+                in_=acc[:, first : first + j1 - j0, :].rearrange("p j d -> p (j d)"),
             )
 
-        def store(kind, b, first, count):
-            result = tiles_of(b, first)[kind]
-            out = ((out_0, out_1), (out_2, out_3))[kind][first // H]
-            to = first % H
-            nc.sync.dma_start(
-                out=out[b, to : to + count].rearrange("h (p j) d -> p h (j d)", j=J),
-                in_=result[:, first % 2 : first % 2 + count, :],
-            )
+        def store(kind, h):
+            result = tiles_of(h)[kind]
+            out = ((out_0, out_1), (out_2, out_3))[kind][h // H]
+            for b in range(B):
+                nc.sync.dma_start(
+                    out=out[b, h % H].rearrange("(p j) d -> p (j d)", j=J), in_=result[b:P:B, :]
+                )
 
-        scalar_copy = nc.scalar.copy
-        vector_copy = nc.vector.tensor_copy
         grouped_of = {}
 
         def flip_tile(tile, group, copy):
             n = group.index(tile)
             if n == 0:
                 grouped_of[group] = new_grouped(len(group))
-            rows = w_rows[tile[1]] if tile[0] == "w" else x_rows[tile[1]][tile[2]]
-            flip(rows, grouped_of[group], n, copy)
+            flip((w_rows if tile[0] == "w" else x_rows)[tile[1]], grouped_of[group], n, copy)
 
         def quantise_group(group):
             name = "_".join(str(part) for tile in group for part in tile)
             made = quantise(grouped_of[group], len(group), name)
             for n in range(len(group)):
-                tile = group[n]
-                if tile[0] == "w":
-                    w_codes[tile[1]] = made[n]
-                else:
-                    x_codes[tile[1]][tile[2]] = made[n]
+                kind, index = group[n]
+                (w_codes if kind == "w" else x_codes)[index] = made[n]
 
-        def w_group(first, count):
-            return tuple(("w", first + n) for n in range(count))
+        def tiles_in(kind, first, count):
+            return tuple((kind, first + n) for n in range(count))
 
-        def x_group(b, first, count):
-            return tuple(("x", b, first + n) for n in range(count))
+        x_groups = [tiles_in("x", j, 1) for j in range(4)] + [tiles_in("x", 4, 2), tiles_in("x", 6, 2)]
+        w_groups = [tiles_in("w", 0, 1), tiles_in("w", 1, 1)] + [tiles_in("w", h, 2) for h in range(2, HEADS, 2)]
 
-        x0 = [x_group(0, j, 1) for j in range(J)]
-        x1 = x_group(1, 0, J)
-        w_groups = [w_group(h, 1) for h in range(4)] + [w_group(4, 2), w_group(6, 2), w_group(8, 4), w_group(12, 4)]
+        def flip_one(kind, index):
+            tile = (kind, index)
+            group = [group for group in x_groups + w_groups if tile in group][0]
+            flip_tile(tile, group, nc.scalar.copy)
 
-        def flip_w(h, copy):
-            group = [group for group in w_groups if ("w", h) in group][0]
-            flip_tile(("w", h), group, copy)
-
-        flip_w(0, scalar_copy)
-        fill_table()
-        flip_tile(x0[0][0], x0[0], vector_copy)
-        flip_tile(x0[1][0], x0[1], scalar_copy)
+        flip_one("w", 0)
+        for j in range(3):
+            flip_one("x", j)
+        fill_table(0)
         quantise_group(w_groups[0])
-        quantise_group(x0[0])
-        flip_tile(x0[2][0], x0[2], vector_copy)
-        quantise_group(x0[1])
-        flip_tile(x0[3][0], x0[3], scalar_copy)
-        first_acc = project(0, 0, (0, 1))
-        flip_w(1, scalar_copy)
-        flip_w(2, scalar_copy)
-        multiply(0, 0, first_acc, 0, 2)
-        flip_w(3, scalar_copy)
-        quantise_group(x0[2])
-        quantise_group(x0[3])
-        second_acc = project(0, 0, (2, 3))
+        quantise_group(x_groups[0])
+        quantise_group(x_groups[1])
+        first_acc = project(0, 0, 2)
+        flip_one("x", 3)
+        quantise_group(x_groups[2])
+        flip_one("w", 1)
+        multiply(0, first_acc, 0, 2)
+        quantise_group(x_groups[3])
+        second_acc = project(0, 2, 4)
+        flip_one("x", 4)
+        flip_one("x", 5)
         quantise_group(w_groups[1])
-        add(nc.vector, 0, 0, 0, 2)
-        flip_w(4, scalar_copy)
-        multiply(0, 0, second_acc, 2, 4)
-        quantise_group(w_groups[2])
-        add(nc.vector, 0, 0, 2, 4)
-        copy_plain(0, 0, first_acc, 0, 2)
-        copy_plain(0, 0, second_acc, 2, 4)
+        accs = {(1, 0): project(1, 0, GROUP)}
+        flip_one("x", 6)
+        flip_one("x", 7)
+        fill_table(1)
+        multiply(0, second_acc, 2, 4)
+        for h in (2, 3):
+            flip_one("w", h)
+        copy_plain(0, first_acc, 0, 2)
+        copy_plain(0, second_acc, 2, 4)
 
-        banks = [(b, h) for b in range(B) for h in range(2 * H)][1:]
-        accs = {}
+        units = [(1, 0), (0, 1), (1, 1)]
+        units += [(h, half) for h in range(2, HEADS) for half in range(2)]
 
-        windows = {
-            1: (w_groups[3], 1),
-            2: (w_groups[4], None),
-            4: (w_groups[5], 3),
-            6: (w_groups[6], 5),
-            10: (w_groups[7], 9),
-            14: (x1, 13),
-        }
-        vector_sums = [(0, 1), (0, 3), (0, 5), (0, 9), (0, 13), (1, 15)]
-        tensor_sums = [(1, 2), (1, 7)]
-        flips = {
-            1: [5],
-            2: [6, 7],
-            3: [8],
-            4: [9, 10],
-            5: [11],
-            6: [12],
-            7: [13],
-            8: [14],
-            9: [15],
-        }
-        x1_flips = {10: 0, 11: 1, 12: 2, 13: 3}
-        added = set()
-        added.add((0, 0))
-        last_pair = [(B - 1, 2 * H - 2), (B - 1, 2 * H - 1)]
-        totals = {}
+        windows = {(1, 0): ([x_groups[4], x_groups[5]], (0, 0)), (0, 1): ([w_groups[2]], None)}
+        for h in range(2, HEADS - 2, 2):
+            windows[(h, 1)] = ([w_groups[h // 2 + 2]], (h, 0))
+        vector_sums = [window[1] for window in windows.values() if window[1] is not None]
+        vector_sums += [(HEADS - 1, 0), (HEADS - 1, 1)]
+        flips = {}
+        for h in range(0, HEADS - 4, 2):
+            flips[(h, 1)] = [("w", h + 4), ("w", h + 5)]
+        plain_done = [(0, 0)]
+        sum_done = []
         later = {}
 
-        def rotated_done(b, h):
-            added.add((b, h))
-            if (b, h) in last_pair:
-                store(1, b, h, 1)
-            elif (b, h - h % 2) in added and (b, h - h % 2 + 1) in added:
-                store(1, b, h - h % 2, 2)
+        def finished(done, unit):
+            done.append(unit)
+            return (unit[0], 0) in done and (unit[0], 1) in done
 
-        def ready(b, h):
-            return w_codes[h] is not None and x_codes[b][J - 1] is not None
+        def ready(h, half):
+            return w_codes[h] is not None and x_codes[(half + 1) * GROUP - 1] is not None
 
         def project_ahead(k):
-            ahead = 2 if banks[k][0] == 0 else 4
-            while len(accs) < len(banks) and len(accs) <= k + ahead and ready(*banks[len(accs)]):
-                b, h = banks[len(accs)]
-                accs[(b, h)] = project(b, h, range(J))
+            while len(accs) < len(units) and len(accs) <= k + 3 and ready(*units[len(accs)]):
+                h, half = units[len(accs)]
+                accs[(h, half)] = project(h, half * GROUP, (half + 1) * GROUP)
 
-        project_ahead(-1)
-        for k in range(len(banks)):
-            b, h = banks[k]
-            if b == 0:
-                for n in flips.get(h, []):
-                    flip_w(n, scalar_copy)
-                if h in x1_flips:
-                    flip_tile(x1[x1_flips[h]], x1, scalar_copy)
-            acc = accs[(b, h)]
-            window = windows.get(h) if b == 0 else None
-            last = k == len(banks) - 1
-            if last:
-                multiply(b, h, acc, 0, 2)
-                multiply(b, h, acc, 2, 4)
-                add(nc.vector, b, h, 0, 2)
-                add(nc.vector, b, h, 2, 4)
-                rotated_done(b, h)
-            elif window is None:
-                multiply(b, h, acc, 0, J)
+        for k in range(len(units)):
+            unit = units[k]
+            h, half = unit
+            j0, j1 = half * GROUP, (half + 1) * GROUP
+            for kind, index in flips.get(unit, []):
+                flip_one(kind, index)
+            if unit in windows:
+                groups, summed = windows[unit]
+                multiply(h, accs[unit], j0, j1 - 1)
+                for group in groups:
+                    quantise_group(group)
+                if summed is not None:
+                    add(nc.vector, summed[0], summed[1] * GROUP, (summed[1] + 1) * GROUP)
+                    if finished(sum_done, summed):
+                        later.setdefault(k + 1, []).append(summed[0])
+                multiply(h, accs[unit], j1 - 1, j1)
             else:
-                multiply(b, h, acc, 0, J - 1)
-                quantise_group(window[0])
-                if window[1] is not None and window[1] != h:
-                    add(nc.vector, b, window[1], 0, J)
-                    rotated_done(b, window[1])
-                multiply(b, h, acc, J - 1, J)
-                if window[1] == h:
-                    add(nc.vector, b, h, 0, J)
-                    rotated_done(b, h)
-            if (b, h) in tensor_sums:
-                later.setdefault(k + 2, []).append((0, b, h))
-                later.setdefault(k + 4, []).append((1, b, h))
-            elif (b, h) not in vector_sums:
-                add(nc.gpsimd, b, h, 0, J)
-                rotated_done(b, h)
+                multiply(h, accs[unit], j0, j1)
+            if unit not in vector_sums:
+                add(nc.gpsimd, h, j0, j1)
+                if finished(sum_done, unit):
+                    later.setdefault(k + 2, []).append(h)
             project_ahead(k)
-            for step, bb, hh in later.get(k, []):
-                if step == 0:
-                    totals[(bb, hh)] = add_on_tensor(bb, hh)
-                else:
-                    rotated = tiles_of(bb, hh)[1]
-                    nc.scalar.copy(out=rotated[:, hh % 2, :], in_=totals[(bb, hh)][:])
-                    rotated_done(bb, hh)
             if k > 0:
-                bb, hh = banks[k - 1]
-                copy_plain(bb, hh, accs[(bb, hh)], 0, J)
-                if (bb, hh) in last_pair:
-                    store(0, bb, hh, 1)
-                elif hh % 2 == 1:
-                    store(0, bb, hh - 1, 2)
-        copy_plain(b, h, acc, 0, J)
-        store(0, b, h, 1)
+                done = units[k - 1]
+                copy_plain(done[0], accs[done], done[1] * GROUP, (done[1] + 1) * GROUP)
+                if finished(plain_done, done):
+                    store(0, done[0])
+            for head in later.get(k, []):
+                store(1, head)
+        for unit in vector_sums[-2:]:
+            add(nc.vector, unit[0], unit[1] * GROUP, (unit[1] + 1) * GROUP)
+        copy_plain(h, accs[(h, half)], j0, j1)
+        for k in range(len(units), len(units) + 2):
+            for head in later.get(k, []):
+                store(1, head)
+        store(0, h)
+        store(1, h)

@@ -27,6 +27,12 @@ HEADS = 2 * H
 FLOPS = 2 * B * T * C * 2 * C
 
 RATIO = 1000.0 ** (-2.0 / DH)
+LOADS = (
+    [("w", 0, 1), ("x", 0, 1), ("x", 1, 1), ("x", 2, 2), ("w", 1, 1), ("w", 2, 1), ("x", 4, 2), ("w", 3, 1), ("x", 6, 2)]
+    + [("w", h, 2) for h in range(4, 16, 2)]
+)
+LAG = 4
+HALVES = 4
 ROUND_MAGIC = 1.5 * 2.0**23
 
 
@@ -36,37 +42,27 @@ def tile_ropeattnlayer_pa_kernel(tc, x, w_qk, out_0, out_1, out_2, out_3):
         const = ctx.enter_context(tc.tile_pool(name="const", bufs=1))
         loaded = ctx.enter_context(tc.tile_pool(name="loaded", bufs=1))
         keep = ctx.enter_context(tc.tile_pool(name="keep", bufs=1))
-        stage = ctx.enter_context(tc.tile_pool(name="stage", bufs=5))
-        results = ctx.enter_context(tc.tile_pool(name="results", bufs=6))
+        stage = ctx.enter_context(tc.tile_pool(name="stage", bufs=4))
+        results = ctx.enter_context(tc.tile_pool(name="results", bufs=4))
         psum = ctx.enter_context(tc.psum_pool(name="psum", bufs=8))
         ctx.enter_context(tc.manual_schedule())
 
         w_view = w_qk.rearrange("(h p) k -> p h k", p=P)
-        w_rows = [None] * HEADS
-        x_rows = [None] * J
+        rows_of = {}
 
-        def load_w(first, count):
-            tile = loaded.tile([P, count, C], BF16, name="w_rows%d" % first)
-            nc.sync.dma_start(out=tile[:], in_=w_view[:, first : first + count, :])
+        def load(kind, first, count):
+            tile = loaded.tile([P, count, C], BF16, name="rows_%s%d" % (kind, first))
+            if kind == "w":
+                nc.sync.dma_start(out=tile[:], in_=w_view[:, first : first + count, :])
+            else:
+                for b in range(B):
+                    positions = x[b].rearrange("(p j) k -> p j k", j=J)
+                    nc.sync.dma_start(out=tile[b:P:B], in_=positions[:, first : first + count, :])
             for n in range(count):
-                w_rows[first + n] = (tile, n)
+                rows_of[(kind, first + n)] = (tile, n)
 
-        def load_x(first, count):
-            tile = loaded.tile([P, count, C], BF16, name="x_rows%d" % first)
-            for b in range(B):
-                positions = x[b].rearrange("(p j) k -> p j k", j=J)
-                nc.sync.dma_start(out=tile[b:P:B], in_=positions[:, first : first + count, :])
-            for n in range(count):
-                x_rows[first + n] = (tile, n)
-
-        load_w(0, 1)
-        load_x(0, 2)
-        load_x(2, 2)
-        load_w(1, 1)
-        load_x(4, 2)
-        load_x(6, 2)
-        for h in range(2, HEADS, 2):
-            load_w(h, 2)
+        for kind, first, count in LOADS:
+            load(kind, first, count)
 
         zero = const.tile([P, 1], F32)
         nc.vector.memset(zero[:], 0.0)
@@ -99,248 +95,253 @@ def tile_ropeattnlayer_pa_kernel(tc, x, w_qk, out_0, out_1, out_2, out_3):
                 nc.vector.tensor_scalar_mul(
                     out=turns[:, :, m * n : (m + 1) * n], in0=turns[:, :, 0:n], scalar1=RATIO ** (m * n)
                 )
-        whole = const.tile([P, J * HALF], F32)
+        span_of = [slice(group * GROUP * HALF, (group + 1) * GROUP * HALF) for group in range(2)]
         flat_turns = turns[:].rearrange("p j i -> p (j i)")
-        nc.vector.tensor_scalar(
-            out=whole[:],
-            in0=flat_turns,
-            scalar1=ROUND_MAGIC,
-            scalar2=ROUND_MAGIC,
-            op0=ALU.add,
-            op1=ALU.subtract,
-        )
-        angles = const.tile([P, 4, J * HALF], F32)
-        nc.vector.tensor_sub(out=angles[:, 1], in0=flat_turns, in1=whole[:])
-        nc.vector.tensor_scalar_mul(out=angles[:, 2], in0=angles[:, 1], scalar1=-1.0)
-        minus_abs = const.tile([P, J * HALF], F32)
-        nc.vector.scalar_tensor_tensor(
-            out=minus_abs[:], in0=angles[:, 1], scalar=-1.0, in1=angles[:, 1], op0=ALU.mult, op1=ALU.min
-        )
-        nc.vector.tensor_scalar_add(out=angles[:, 0], in0=minus_abs[:], scalar1=0.25)
-        nc.vector.tensor_scalar_add(out=angles[:, 3], in0=minus_abs[:], scalar1=0.25)
+        table = const.tile([P, 2, 2, BANK], F32)
 
-        table = const.tile([P, 2, J * HALF, 2], F32)
+        angles_of = {}
 
-        def fill_table(group):
-            span = slice(group * GROUP * HALF, (group + 1) * GROUP * HALF)
-            nc.scalar.activation(
-                out=table[:, :, span, :],
-                in_=angles[:, :, span].rearrange("p (q f) n -> p q n f", q=2),
-                func=ACT.Sin,
-                scale=2.0 * math.pi,
+        def wrap_angles(group):
+            whole = const.tile([P, BANK // 2], F32, name="whole%d" % group)
+            nc.vector.tensor_scalar(
+                out=whole[:],
+                in0=flat_turns[:, span_of[group]],
+                scalar1=ROUND_MAGIC,
+                scalar2=ROUND_MAGIC,
+                op0=ALU.add,
+                op1=ALU.subtract,
             )
+            angles = const.tile([P, 3, BANK // 2], F32, name="angles%d" % group)
+            nc.vector.tensor_sub(out=angles[:, 2], in0=flat_turns[:, span_of[group]], in1=whole[:])
+            nc.vector.tensor_scalar_mul(out=angles[:, 0], in0=angles[:, 2], scalar1=-1.0)
+            angles_of[group] = angles
 
-        x_codes = [None] * J
-        w_codes = [None] * HEADS
+        def cosine_angles(group):
+            angles = angles_of[group]
+            minus_abs = const.tile([P, BANK // 2], F32, name="minus_abs%d" % group)
+            nc.vector.tensor_tensor(out=minus_abs[:], in0=angles[:, 0], in1=angles[:, 2], op=ALU.min)
+            nc.vector.tensor_scalar_add(out=angles[:, 1], in0=minus_abs[:], scalar1=0.25)
 
-        def flip(source, grouped, n, copy):
-            rows, m = source
+        def fill_table(group, part):
+            columns = slice(part * BANK // 2, (part + 1) * BANK // 2)
+            half_columns = slice(part * BANK // 4, (part + 1) * BANK // 4)
+            for q in range(2):
+                nc.scalar.activation(
+                    out=table[:, group, q, columns].rearrange("p (n f) -> p n f", f=2),
+                    in_=angles_of[group][:, 1 - q : 3 - q, half_columns].rearrange("p f n -> p n f"),
+                    func=ACT.Sin,
+                    scale=2.0 * math.pi,
+                )
+
+        codes_of = {}
+        grouped_of = {}
+
+        def flip(kind, index, engine_copy):
+            rows, m = rows_of[(kind, index)]
             words = rows[:, m, :].bitcast(F32)
             flipped = psum.tile([P, PASSES, 2, P], F32, name="flipped", tag="bank")
             for g in range(PASSES):
                 for u in range(2):
                     every_second = slice(2 * P * g + u, 2 * P * (g + 1), 2)
                     nc.tensor.transpose(flipped[:, g, u, :], words[:, every_second], ident[:])
-            copy(
-                out=grouped[:, n, :].bitcast(F32).rearrange("p (g r u) -> p g r u", g=PASSES, u=2),
+            grouped = stage.tile([P, PASSES * P * PACK], BF16, name="grouped", tag="grouped", align_bytes=64)
+            grouped_of[(kind, index)] = grouped
+            engine_copy(
+                out=grouped[:].bitcast(F32).rearrange("p (g r u) -> p g r u", g=PASSES, u=2),
                 in_=flipped[:].rearrange("p g u r -> p g r u"),
             )
 
-        def new_grouped(tiles):
-            return stage.tile(
-                [P, tiles, PASSES * P * PACK], BF16, name="grouped", tag="grouped", align_bytes=64
-            )
-
-        def quantise(grouped, tiles, name):
-            codes = keep.tile([P, tiles, PASSES, P], U32, name=name + "_codes", align_bytes=64)
-            scales = keep.tile([P, tiles, PASSES, P], U8, name=name + "_scales", align_bytes=64)
+        def quantise(kind, index):
+            name = "%s%d" % (kind, index)
+            codes = keep.tile([P, PASSES, P], U32, name=name + "_codes", align_bytes=64)
+            scales = keep.tile([P, PASSES, P], U8, name=name + "_scales", align_bytes=64)
             nc.vector.quantize_mx(
-                out=codes[:].rearrange("p n g r -> p (n g r)").bitcast(FP8X4),
-                scales=scales[:].rearrange("p n g r -> p (n g r)"),
-                in_=grouped[:].rearrange("p n c -> p (n c)"),
+                out=codes[:].rearrange("p g r -> p (g r)").bitcast(FP8X4),
+                scales=scales[:].rearrange("p g r -> p (g r)"),
+                in_=grouped_of[(kind, index)][:],
             )
-            return [(codes[:, n], scales[:, n]) for n in range(tiles)]
+            codes_of[(kind, index)] = (codes, scales)
 
-        def project(h, j0, j1):
+        accs = {}
+
+        def project(unit):
+            h, half, j0, j1 = unit
             acc = psum.tile([P, GROUP, DH], F32, name="acc", tag="bank")
+            accs[unit] = acc
+            w_codes, w_scales = codes_of[("w", h)]
             for j in range(j0, j1):
+                x_codes, x_scales = codes_of[("x", half * GROUP + j)]
                 for g in range(PASSES):
                     nc.tensor.matmul_mx(
-                        out=acc[:, j % GROUP, :],
-                        lhsT=x_codes[j][0][:, g, :].bitcast(FP8X4),
-                        lhsT_scale=x_codes[j][1][:, g, :],
-                        rhs=w_codes[h][0][:, g, :].bitcast(FP8X4),
-                        rhs_scale=w_codes[h][1][:, g, :],
+                        out=acc[:, j, :],
+                        lhsT=x_codes[:, g, :].bitcast(FP8X4),
+                        lhsT_scale=x_scales[:, g, :],
+                        rhs=w_codes[:, g, :].bitcast(FP8X4),
+                        rhs_scale=w_scales[:, g, :],
                         start=(g == 0),
                         stop=(g == PASSES - 1),
                     )
-            return acc
 
-        results_of = {}
+        plain_of = {}
+        rotated_of = {}
+        products_of = {}
 
-        def tiles_of(h):
-            if h not in results_of:
-                plain = results.tile([P, J * DH], F32, name="plain", tag="plain")
-                rotated = results.tile([P, J * DH], F32, name="rotated", tag="rotated")
-                products = results.tile([P, 2, 2, BANK], F32, name="products", tag="products")
-                results_of[h] = (plain, rotated, products)
-            return results_of[h]
+        def plain_tile(h):
+            if h not in plain_of:
+                plain_of[h] = results.tile([P, 2, BANK], F32, name="plain", tag="plain")
+            return plain_of[h][:]
 
-        def multiply(h, acc, j0, j1):
-            products = tiles_of(h)[2][:, j0 // GROUP]
+        def rotated_tile(h):
+            if h < LAG:
+                if h // 2 not in rotated_of:
+                    rotated_of[h // 2] = const.tile([P, 2, 2, BANK], F32, name="first_rotated%d" % (h // 2))
+                return rotated_of[h // 2][:, :, h % 2]
+            if h not in rotated_of:
+                rotated_of[h] = results.tile([P, 2, BANK], F32, name="rotated", tag="rotated")
+            return rotated_of[h][:]
+
+        def pair_of(h, half):
+            if h < LAG:
+                return (h // 2, half), h % 2
+            return (h, 2), half
+
+        def product(unit):
+            h, half, j0, j1 = unit
+            key, place = pair_of(h, half)
+            if key not in products_of:
+                products_of[key] = stage.tile([P, 2, 2, BANK], F32, name="products", tag="products")
             n = (j1 - j0) * HALF
-            first = j0 % GROUP
-            span = slice(first * DH, (first + j1 - j0) * DH)
-            by_parity = acc[:, first : first + j1 - j0, :].rearrange("p j (i q) -> p q (j i)", q=2)
+            span = slice(j0 * DH, j1 * DH)
+            values = accs[unit][:, j0:j1, :].rearrange("p j (i q) -> p q (j i)", q=2)
             nc.vector.tensor_tensor(
-                out=products[:, :, span].rearrange("p q (n f) -> p q n f", f=2),
-                in0=by_parity.unsqueeze(3).to_broadcast([P, 2, n, 2]),
-                in1=table[:, :, j0 * HALF : j1 * HALF, :],
+                out=products_of[key][:, place, :, span].rearrange("p q (n f) -> p q n f", f=2),
+                in0=values.unsqueeze(3).to_broadcast([P, 2, n, 2]),
+                in1=table[:, half, :, span].rearrange("p q (n f) -> p q n f", f=2),
                 op=ALU.mult,
             )
 
-        def add(engine, h, j0, j1):
-            plain, rotated, products = tiles_of(h)
-            half = j0 // GROUP
-            span = slice((j0 - half * GROUP) * DH, (j1 - half * GROUP) * DH)
-            engine.tensor_tensor(
-                out=rotated[:, j0 * DH : j1 * DH],
-                in0=products[:, half, 0, span],
-                in1=products[:, half, 1, span],
-                op=ALU.add,
-            )
-
-        def copy_plain(h, acc, j0, j1):
-            plain = tiles_of(h)[0]
-            first = j0 % GROUP
-            nc.scalar.copy(
-                out=plain[:, j0 * DH : j1 * DH],
-                in_=acc[:, first : first + j1 - j0, :].rearrange("p j d -> p (j d)"),
-            )
-
-        def store(kind, h):
-            result = tiles_of(h)[kind]
-            out = ((out_0, out_1), (out_2, out_3))[kind][h // H]
-            for b in range(B):
-                nc.sync.dma_start(
-                    out=out[b, h % H].rearrange("(p j) d -> p (j d)", j=J), in_=result[b:P:B, :]
-                )
-
-        grouped_of = {}
-
-        def flip_tile(tile, group, copy):
-            n = group.index(tile)
-            if n == 0:
-                grouped_of[group] = new_grouped(len(group))
-            flip((w_rows if tile[0] == "w" else x_rows)[tile[1]], grouped_of[group], n, copy)
-
-        def quantise_group(group):
-            name = "_".join(str(part) for tile in group for part in tile)
-            made = quantise(grouped_of[group], len(group), name)
-            for n in range(len(group)):
-                kind, index = group[n]
-                (w_codes if kind == "w" else x_codes)[index] = made[n]
-
-        def tiles_in(kind, first, count):
-            return tuple((kind, first + n) for n in range(count))
-
-        x_groups = [tiles_in("x", j, 1) for j in range(4)] + [tiles_in("x", 4, 2), tiles_in("x", 6, 2)]
-        w_groups = [tiles_in("w", 0, 1), tiles_in("w", 1, 1)] + [tiles_in("w", h, 2) for h in range(2, HEADS, 2)]
-
-        def flip_one(kind, index):
-            tile = (kind, index)
-            group = [group for group in x_groups + w_groups if tile in group][0]
-            flip_tile(tile, group, nc.scalar.copy)
-
-        flip_one("w", 0)
-        for j in range(3):
-            flip_one("x", j)
-        fill_table(0)
-        quantise_group(w_groups[0])
-        quantise_group(x_groups[0])
-        quantise_group(x_groups[1])
-        first_acc = project(0, 0, 2)
-        flip_one("x", 3)
-        quantise_group(x_groups[2])
-        flip_one("w", 1)
-        multiply(0, first_acc, 0, 2)
-        quantise_group(x_groups[3])
-        second_acc = project(0, 2, 4)
-        flip_one("x", 4)
-        flip_one("x", 5)
-        quantise_group(w_groups[1])
-        accs = {(1, 0): project(1, 0, GROUP)}
-        flip_one("x", 6)
-        flip_one("x", 7)
-        fill_table(1)
-        multiply(0, second_acc, 2, 4)
-        for h in (2, 3):
-            flip_one("w", h)
-        copy_plain(0, first_acc, 0, 2)
-        copy_plain(0, second_acc, 2, 4)
-
-        units = [(1, 0), (0, 1), (1, 1)]
-        units += [(h, half) for h in range(2, HEADS) for half in range(2)]
-
-        windows = {(1, 0): ([x_groups[4], x_groups[5]], (0, 0)), (0, 1): ([w_groups[2]], None)}
-        for h in range(2, HEADS - 2, 2):
-            windows[(h, 1)] = ([w_groups[h // 2 + 2]], (h, 0))
-        vector_sums = [window[1] for window in windows.values() if window[1] is not None]
-        vector_sums += [(HEADS - 1, 0), (HEADS - 1, 1)]
-        flips = {}
-        for h in range(0, HEADS - 4, 2):
-            flips[(h, 1)] = [("w", h + 4), ("w", h + 5)]
-        plain_done = [(0, 0)]
-        sum_done = []
-        later = {}
-
-        def finished(done, unit):
-            done.append(unit)
-            return (unit[0], 0) in done and (unit[0], 1) in done
-
-        def ready(h, half):
-            return w_codes[h] is not None and x_codes[(half + 1) * GROUP - 1] is not None
-
-        def project_ahead(k):
-            while len(accs) < len(units) and len(accs) <= k + 3 and ready(*units[len(accs)]):
-                h, half = units[len(accs)]
-                accs[(h, half)] = project(h, half * GROUP, (half + 1) * GROUP)
-
-        for k in range(len(units)):
-            unit = units[k]
-            h, half = unit
-            j0, j1 = half * GROUP, (half + 1) * GROUP
-            for kind, index in flips.get(unit, []):
-                flip_one(kind, index)
-            if unit in windows:
-                groups, summed = windows[unit]
-                multiply(h, accs[unit], j0, j1 - 1)
-                for group in groups:
-                    quantise_group(group)
-                if summed is not None:
-                    add(nc.vector, summed[0], summed[1] * GROUP, (summed[1] + 1) * GROUP)
-                    if finished(sum_done, summed):
-                        later.setdefault(k + 1, []).append(summed[0])
-                multiply(h, accs[unit], j1 - 1, j1)
+        def total(engine, h, half, n0=0, n1=2):
+            key, place = pair_of(h, half)
+            products = products_of[key]
+            if h < LAG:
+                rotated_tile(h)
+                out = rotated_of[h // 2][:, half, n0:n1]
             else:
-                multiply(h, accs[unit], j0, j1)
-            if unit not in vector_sums:
-                add(nc.gpsimd, h, j0, j1)
-                if finished(sum_done, unit):
-                    later.setdefault(k + 2, []).append(h)
-            project_ahead(k)
-            if k > 0:
-                done = units[k - 1]
-                copy_plain(done[0], accs[done], done[1] * GROUP, (done[1] + 1) * GROUP)
-                if finished(plain_done, done):
-                    store(0, done[0])
-            for head in later.get(k, []):
-                store(1, head)
-        for unit in vector_sums[-2:]:
-            add(nc.vector, unit[0], unit[1] * GROUP, (unit[1] + 1) * GROUP)
-        copy_plain(h, accs[(h, half)], j0, j1)
-        for k in range(len(units), len(units) + 2):
-            for head in later.get(k, []):
-                store(1, head)
-        store(0, h)
-        store(1, h)
+                out = rotated_tile(h)[:, n0:n1]
+            engine.tensor_tensor(out=out, in0=products[:, n0:n1, 0], in1=products[:, n0:n1, 1], op=ALU.add)
+
+        def copy_plain(unit):
+            h, half, j0, j1 = unit
+            nc.scalar.copy(
+                out=plain_tile(h)[:, half, j0 * DH : j1 * DH],
+                in_=accs[unit][:, j0:j1, :].rearrange("p j d -> p (j d)"),
+            )
+
+        def store(kind, h, half=None):
+            out = ((out_0, out_1), (out_2, out_3))[kind][h // H]
+            result = rotated_tile(h) if kind else plain_tile(h)
+            for b in range(B):
+                rows = out[b, h % H].rearrange("(p n j) d -> p n (j d)", n=2, j=GROUP)
+                if half is None:
+                    nc.sync.dma_start(out=rows, in_=result[b:P:B])
+                else:
+                    nc.sync.dma_start(out=rows[:, half], in_=result[b:P:B, half])
+
+        def U(h, half, j0=0, j1=GROUP):
+            return (h, half, j0, j1)
+
+        SC = nc.scalar.copy
+        VC = nc.vector.tensor_copy
+        wrap_angles(0)
+        cosine_angles(0)
+        wrap_angles(1)
+        fill_table(0, 0)
+        flip("w", 0, SC)
+        flip("x", 0, VC)
+        flip("x", 1, SC)
+        quantise("x", 0)
+        quantise("w", 0)
+        flip("x", 2, SC)
+        quantise("x", 1)
+        flip("x", 3, VC)
+        fill_table(0, 1)
+        flip("w", 1, SC)
+        project(U(0, 0, 0, 2))
+        flip("w", 2, SC)
+        quantise("x", 2)
+        quantise("x", 3)
+        product(U(0, 0, 0, 2))
+        flip("x", 4, SC)
+        project(U(0, 0, 2, 4))
+        quantise("w", 1)
+        cosine_angles(1)
+        copy_plain(U(0, 0, 0, 2))
+        product(U(0, 0, 2, 4))
+        flip("x", 5, SC)
+        project(U(1, 0))
+        copy_plain(U(0, 0, 2, 4))
+        quantise("w", 2)
+        quantise("x", 4)
+        total(nc.gpsimd, 0, 0, 0, 1)
+        flip("w", 3, SC)
+        flip("x", 6, SC)
+        project(U(2, 0))
+        product(U(1, 0))
+        quantise("x", 5)
+        quantise("w", 3)
+        total(nc.gpsimd, 0, 0, 1, 2)
+        copy_plain(U(1, 0))
+        flip("x", 7, SC)
+        store(0, 0, 0)
+        store(0, 1, 0)
+        store(1, 0, 0)
+        store(1, 1, 0)
+        product(U(2, 0))
+        project(U(3, 0))
+        quantise("x", 6)
+        quantise("x", 7)
+        project(U(0, 1))
+        fill_table(1, 0)
+        fill_table(1, 1)
+        copy_plain(U(2, 0))
+        flip("w", 4, SC)
+        product(U(3, 0))
+        total(nc.gpsimd, 2, 0)
+        project(U(1, 1))
+        copy_plain(U(3, 0))
+        store(0, 2, 0)
+        store(0, 3, 0)
+        store(1, 2, 0)
+        store(1, 3, 0)
+        flip("w", 5, SC)
+
+        pairs = [((h, 1), (h + 1, 1)) for h in range(0, LAG, 2)] + [((h, 0), (h, 1)) for h in range(LAG, HEADS)]
+        end = len(pairs) - 1
+
+        def store_pair(kind, pair):
+            for h in sorted(set(unit[0] for unit in pair)):
+                store(kind, h, 1 if h < HALVES else None)
+
+        for s in range(len(pairs)):
+            first, second = pairs[s]
+            single = s >= end - 1
+            product(U(*first))
+            if single:
+                total(nc.gpsimd, first[0], first[1], 0, 1)
+            product(U(*second))
+            h = LAG + s
+            if h < HEADS:
+                quantise("w", h)
+            if h + 2 < HEADS:
+                flip("w", h + 2, SC)
+            for unit in pairs[s + 1] if s < end else []:
+                if U(*unit) not in accs:
+                    project(U(*unit))
+            if single:
+                total(nc.vector if s == end else nc.gpsimd, first[0], first[1], 1, 2)
+            else:
+                total(nc.gpsimd, first[0], first[1])
+            for unit in pairs[s]:
+                copy_plain(U(*unit))
+            store_pair(0, pairs[s])
+            store_pair(1, pairs[s])

import math
from contextlib import ExitStack

import concourse.masks as masks
import concourse.mybir as mybir

F32 = mybir.dt.float32
BF16 = mybir.dt.bfloat16
I32 = mybir.dt.int32
U32 = mybir.dt.uint32
U8 = mybir.dt.uint8
FP8X4 = mybir.dt.float8_e4m3fn_x4
ALU = mybir.AluOpType
ACT = mybir.ActivationFunctionType

B, T, C, H, DH = 2, 512, 1024, 8, 128
P = 128
PACK = 4
PASSES = C // (P * PACK)
ROWS = P // B
J = T // ROWS
GROUP = J // 2
HALF = DH // 2
BANK = GROUP * DH
HEADS = 2 * H

FLOPS = 2 * B * T * C * 2 * C

RATIO = 1000.0 ** (-2.0 / DH)
LOADS = (
    [("w", 0, 1), ("x", 0, 1), ("x", 1, 1), ("x", 2, 2), ("w", 1, 1), ("w", 2, 1), ("x", 4, 2), ("w", 3, 1), ("x", 6, 2)]
    + [("w", h, 2) for h in range(4, 16, 2)]
)
LAG = 4
HALVES = 4
ROUND_MAGIC = 1.5 * 2.0**23


def tile_ropeattnlayer_pa_kernel(tc, x, w_qk, out_0, out_1, out_2, out_3):
    nc = tc.nc
    with ExitStack() as ctx:
        const = ctx.enter_context(tc.tile_pool(name="const", bufs=1))
        loaded = ctx.enter_context(tc.tile_pool(name="loaded", bufs=1))
        keep = ctx.enter_context(tc.tile_pool(name="keep", bufs=1))
        stage = ctx.enter_context(tc.tile_pool(name="stage", bufs=4))
        results = ctx.enter_context(tc.tile_pool(name="results", bufs=4))
        psum = ctx.enter_context(tc.psum_pool(name="psum", bufs=8))
        ctx.enter_context(tc.manual_schedule())

        w_view = w_qk.rearrange("(h p) k -> p h k", p=P)
        rows_of = {}

        def load(kind, first, count):
            tile = loaded.tile([P, count, C], BF16, name="rows_%s%d" % (kind, first))
            if kind == "w":
                nc.sync.dma_start(out=tile[:], in_=w_view[:, first : first + count, :])
            else:
                for b in range(B):
                    positions = x[b].rearrange("(p j) k -> p j k", j=J)
                    nc.sync.dma_start(out=tile[b:P:B], in_=positions[:, first : first + count, :])
            for n in range(count):
                rows_of[(kind, first + n)] = (tile, n)

        for kind, first, count in LOADS:
            load(kind, first, count)

        zero = const.tile([P, 1], F32)
        nc.vector.memset(zero[:], 0.0)
        warm = const.tile([P, 1], F32)
        nc.scalar.activation(out=warm[:], in_=zero[:], func=ACT.Sin)

        four_p = const.tile([P, 1], I32)
        nc.gpsimd.iota(four_p[:], pattern=[[0, 1]], base=0, channel_multiplier=4)
        tile_number = const.tile([P, J], F32)
        nc.gpsimd.iota(
            tile_number[:], pattern=[[1, J]], base=1, channel_multiplier=0, allow_small_or_imprecise_dtypes=True
        )
        ident = const.tile([P, P], F32)
        masks.make_identity(nc, ident[:])
        first_int = const.tile([P, 1], I32)
        nc.vector.tensor_single_scalar(out=first_int[:], in_=four_p[:], scalar=T - J, op=ALU.bitwise_and)
        first_position = const.tile([P, 1], F32)
        nc.vector.tensor_copy(out=first_position[:], in_=first_int[:])
        turns = const.tile([P, J, HALF], F32)
        nc.vector.tensor_scalar(
            out=turns[:, :, 0:1],
            in0=tile_number[:].unsqueeze(2),
            scalar1=first_position[:],
            scalar2=RATIO / (2.0 * math.pi),
            op0=ALU.add,
            op1=ALU.mult,
        )
        for n in (1, 4, 16):
            for m in range(1, 4):
                nc.vector.tensor_scalar_mul(
                    out=turns[:, :, m * n : (m + 1) * n], in0=turns[:, :, 0:n], scalar1=RATIO ** (m * n)
                )
        span_of = [slice(group * GROUP * HALF, (group + 1) * GROUP * HALF) for group in range(2)]
        flat_turns = turns[:].rearrange("p j i -> p (j i)")
        table = const.tile([P, 2, 2, BANK], F32)

        angles_of = {}

        def wrap_angles(group):
            whole = const.tile([P, BANK // 2], F32, name="whole%d" % group)
            nc.vector.tensor_scalar(
                out=whole[:],
                in0=flat_turns[:, span_of[group]],
                scalar1=ROUND_MAGIC,
                scalar2=ROUND_MAGIC,
                op0=ALU.add,
                op1=ALU.subtract,
            )
            angles = const.tile([P, 3, BANK // 2], F32, name="angles%d" % group)
            nc.vector.tensor_sub(out=angles[:, 2], in0=flat_turns[:, span_of[group]], in1=whole[:])
            nc.vector.tensor_scalar_mul(out=angles[:, 0], in0=angles[:, 2], scalar1=-1.0)
            angles_of[group] = angles

        def cosine_angles(group):
            angles = angles_of[group]
            minus_abs = const.tile([P, BANK // 2], F32, name="minus_abs%d" % group)
            nc.vector.tensor_tensor(out=minus_abs[:], in0=angles[:, 0], in1=angles[:, 2], op=ALU.min)
            nc.vector.tensor_scalar_add(out=angles[:, 1], in0=minus_abs[:], scalar1=0.25)

        def fill_table(group, part):
            columns = slice(part * BANK // 2, (part + 1) * BANK // 2)
            half_columns = slice(part * BANK // 4, (part + 1) * BANK // 4)
            for q in range(2):
                nc.scalar.activation(
                    out=table[:, group, q, columns].rearrange("p (n f) -> p n f", f=2),
                    in_=angles_of[group][:, 1 - q : 3 - q, half_columns].rearrange("p f n -> p n f"),
                    func=ACT.Sin,
                    scale=2.0 * math.pi,
                )

        codes_of = {}
        grouped_of = {}

        def flip(kind, index, engine_copy):
            rows, m = rows_of[(kind, index)]
            words = rows[:, m, :].bitcast(F32)
            flipped = psum.tile([P, PASSES, 2, P], F32, name="flipped", tag="bank")
            for g in range(PASSES):
                for u in range(2):
                    every_second = slice(2 * P * g + u, 2 * P * (g + 1), 2)
                    nc.tensor.transpose(flipped[:, g, u, :], words[:, every_second], ident[:])
            grouped = stage.tile([P, PASSES * P * PACK], BF16, name="grouped", tag="grouped", align_bytes=64)
            grouped_of[(kind, index)] = grouped
            engine_copy(
                out=grouped[:].bitcast(F32).rearrange("p (g r u) -> p g r u", g=PASSES, u=2),
                in_=flipped[:].rearrange("p g u r -> p g r u"),
            )

        def quantise(kind, index):
            name = "%s%d" % (kind, index)
            codes = keep.tile([P, PASSES, P], U32, name=name + "_codes", align_bytes=64)
            scales = keep.tile([P, PASSES, P], U8, name=name + "_scales", align_bytes=64)
            nc.vector.quantize_mx(
                out=codes[:].rearrange("p g r -> p (g r)").bitcast(FP8X4),
                scales=scales[:].rearrange("p g r -> p (g r)"),
                in_=grouped_of[(kind, index)][:],
            )
            codes_of[(kind, index)] = (codes, scales)

        accs = {}

        def project(unit):
            h, half, j0, j1 = unit
            acc = psum.tile([P, GROUP, DH], F32, name="acc", tag="bank")
            accs[unit] = acc
            w_codes, w_scales = codes_of[("w", h)]
            for j in range(j0, j1):
                x_codes, x_scales = codes_of[("x", half * GROUP + j)]
                for g in range(PASSES):
                    nc.tensor.matmul_mx(
                        out=acc[:, j, :],
                        lhsT=x_codes[:, g, :].bitcast(FP8X4),
                        lhsT_scale=x_scales[:, g, :],
                        rhs=w_codes[:, g, :].bitcast(FP8X4),
                        rhs_scale=w_scales[:, g, :],
                        start=(g == 0),
                        stop=(g == PASSES - 1),
                    )

        plain_of = {}
        rotated_of = {}
        products_of = {}

        def plain_tile(h):
            if h not in plain_of:
                plain_of[h] = results.tile([P, 2, BANK], F32, name="plain", tag="plain")
            return plain_of[h][:]

        def rotated_tile(h):
            if h < LAG:
                if h // 2 not in rotated_of:
                    rotated_of[h // 2] = const.tile([P, 2, 2, BANK], F32, name="first_rotated%d" % (h // 2))
                return rotated_of[h // 2][:, :, h % 2]
            if h not in rotated_of:
                rotated_of[h] = results.tile([P, 2, BANK], F32, name="rotated", tag="rotated")
            return rotated_of[h][:]

        def pair_of(h, half):
            if h < LAG:
                return (h // 2, half), h % 2
            return (h, 2), half

        def product(unit):
            h, half, j0, j1 = unit
            key, place = pair_of(h, half)
            if key not in products_of:
                products_of[key] = stage.tile([P, 2, 2, BANK], F32, name="products", tag="products")
            n = (j1 - j0) * HALF
            span = slice(j0 * DH, j1 * DH)
            values = accs[unit][:, j0:j1, :].rearrange("p j (i q) -> p q (j i)", q=2)
            nc.vector.tensor_tensor(
                out=products_of[key][:, place, :, span].rearrange("p q (n f) -> p q n f", f=2),
                in0=values.unsqueeze(3).to_broadcast([P, 2, n, 2]),
                in1=table[:, half, :, span].rearrange("p q (n f) -> p q n f", f=2),
                op=ALU.mult,
            )

        def total(engine, h, half, n0=0, n1=2):
            key, place = pair_of(h, half)
            products = products_of[key]
            if h < LAG:
                rotated_tile(h)
                out = rotated_of[h // 2][:, half, n0:n1]
            else:
                out = rotated_tile(h)[:, n0:n1]
            engine.tensor_tensor(out=out, in0=products[:, n0:n1, 0], in1=products[:, n0:n1, 1], op=ALU.add)

        def copy_plain(unit):
            h, half, j0, j1 = unit
            nc.scalar.copy(
                out=plain_tile(h)[:, half, j0 * DH : j1 * DH],
                in_=accs[unit][:, j0:j1, :].rearrange("p j d -> p (j d)"),
            )

        def store(kind, h, half=None):
            out = ((out_0, out_1), (out_2, out_3))[kind][h // H]
            result = rotated_tile(h) if kind else plain_tile(h)
            for b in range(B):
                rows = out[b, h % H].rearrange("(p n j) d -> p n (j d)", n=2, j=GROUP)
                if half is None:
                    nc.sync.dma_start(out=rows, in_=result[b:P:B])
                else:
                    nc.sync.dma_start(out=rows[:, half], in_=result[b:P:B, half])

        def U(h, half, j0=0, j1=GROUP):
            return (h, half, j0, j1)

        SC = nc.scalar.copy
        VC = nc.vector.tensor_copy
        wrap_angles(0)
        cosine_angles(0)
        wrap_angles(1)
        fill_table(0, 0)
        flip("w", 0, SC)
        flip("x", 0, VC)
        flip("x", 1, SC)
        quantise("x", 0)
        quantise("w", 0)
        flip("x", 2, SC)
        quantise("x", 1)
        flip("x", 3, VC)
        fill_table(0, 1)
        flip("w", 1, SC)
        project(U(0, 0, 0, 2))
        flip("w", 2, SC)
        quantise("x", 2)
        quantise("x", 3)
        product(U(0, 0, 0, 2))
        flip("x", 4, SC)
        project(U(0, 0, 2, 4))
        quantise("w", 1)
        cosine_angles(1)
        copy_plain(U(0, 0, 0, 2))
        product(U(0, 0, 2, 4))
        flip("x", 5, SC)
        project(U(1, 0))
        copy_plain(U(0, 0, 2, 4))
        quantise("w", 2)
        quantise("x", 4)
        total(nc.gpsimd, 0, 0, 0, 1)
        flip("w", 3, SC)
        flip("x", 6, SC)
        project(U(2, 0))
        product(U(1, 0))
        quantise("x", 5)
        quantise("w", 3)
        total(nc.gpsimd, 0, 0, 1, 2)
        copy_plain(U(1, 0))
        flip("x", 7, SC)
        store(0, 0, 0)
        store(0, 1, 0)
        store(1, 0, 0)
        store(1, 1, 0)
        product(U(2, 0))
        project(U(3, 0))
        quantise("x", 6)
        quantise("x", 7)
        project(U(0, 1))
        fill_table(1, 0)
        fill_table(1, 1)
        copy_plain(U(2, 0))
        flip("w", 4, SC)
        product(U(3, 0))
        total(nc.gpsimd, 2, 0)
        project(U(1, 1))
        copy_plain(U(3, 0))
        store(0, 2, 0)
        store(0, 3, 0)
        store(1, 2, 0)
        store(1, 3, 0)
        flip("w", 5, SC)

        pairs = [((h, 1), (h + 1, 1)) for h in range(0, LAG, 2)] + [((h, 0), (h, 1)) for h in range(LAG, HEADS)]
        end = len(pairs) - 1

        def store_pair(kind, pair):
            for h in sorted(set(unit[0] for unit in pair)):
                store(kind, h, 1 if h < HALVES else None)

        for s in range(len(pairs)):
            first, second = pairs[s]
            single = s >= end - 1
            product(U(*first))
            if single:
                total(nc.gpsimd, first[0], first[1], 0, 1)
            product(U(*second))
            h = LAG + s
            if h < HEADS:
                quantise("w", h)
            if h + 2 < HEADS:
                flip("w", h + 2, SC)
            for unit in pairs[s + 1] if s < end else []:
                if U(*unit) not in accs:
                    project(U(*unit))
            if single:
                total(nc.vector if s == end else nc.gpsimd, first[0], first[1], 1, 2)
            else:
                total(nc.gpsimd, first[0], first[1])
            for unit in pairs[s]:
                copy_plain(U(*unit))
            store_pair(0, pairs[s])
            store_pair(1, pairs[s])
